import numpy as np
import ml_dtypes


def mxq(x, axis, fmt="e4m3"):
    dtype, down = {"e4m3": (ml_dtypes.float8_e4m3fn, 7), "e5m2": (ml_dtypes.float8_e5m2, 14)}[fmt]
    v = np.moveaxis(np.asarray(x, np.float32).astype(ml_dtypes.bfloat16).astype(np.float64), axis, -1)
    blocks = v.reshape(v.shape[:-1] + (-1, 32))
    amax = np.abs(blocks).max(-1, keepdims=True)
    byte = np.maximum(np.where(amax > 0, np.frexp(amax)[1] - 1 + 127, 0) - down, 1)
    scale = np.exp2(byte - 127.0)
    codes = (blocks / scale).astype(np.float32).astype(dtype).astype(np.float64)
    return np.moveaxis((codes * scale).reshape(v.shape), -1, axis)


WIDE = False


def mx_kscale(k):
    if not WIDE:
        return np.ones(k)
    levels = np.array([10, -10, 5, -5, 0])
    a = np.random.permutation(np.resize(levels, k // 512 * 4)).reshape(k // 512, 4)
    idx = np.arange(k)
    return np.exp2(a[idx // 512, idx % 128 // 32])


BF16 = ml_dtypes.bfloat16


def bf(x):
    return np.asarray(x, np.float32).astype(BF16)


def f64(x):
    return np.asarray(x).astype(np.float64)


E2M1 = np.array([0.0, 0.5, 1.0, 1.5, 2.0, 3.0, 4.0, 6.0, -0.0, -0.5, -1.0, -1.5, -2.0, -3.0, -4.0, -6.0])


def pack_weight(w, fmt):
    k, n = w.shape
    w = f64(bf(w)).reshape(k // 32, 32, n)
    amax = np.abs(w).max(1)
    if fmt == "e4m3":
        byte = np.frexp(amax)[1] - 1 + 127 - 7
    else:
        mant, ex = np.frexp(amax / 6.0)
        byte = np.where(mant > 0.5, ex, ex - 1) + 127
    byte = np.clip(np.where(amax > 0, byte, 1), 1, 254)
    scaled = (w * np.exp2(127.0 - byte)[:, None, :]).reshape(k, n).astype(np.float32)
    by_word = np.ascontiguousarray(scaled.reshape(k // 512, 128, 4, n).transpose(0, 1, 3, 2))
    if fmt == "e4m3":
        words = by_word.astype(ml_dtypes.float8_e4m3fn).view(np.uint8)
    else:
        c = by_word.astype(ml_dtypes.float4_e2m1fn).view(np.uint8) & 0xF
        words = c[..., 0::2] | (c[..., 1::2] << 4)
    return np.ascontiguousarray(words), np.ascontiguousarray(byte.astype(np.uint8).reshape(k // 512, 16, n))


def unpack_weight(words, scales, fmt):
    g, p, n, _ = words.shape
    if fmt == "e4m3":
        vals = np.ascontiguousarray(words).view(ml_dtypes.float8_e4m3fn).astype(np.float64)
    else:
        nib = np.empty((g, p, n, 4), np.uint8)
        nib[..., 0::2] = words & 0xF
        nib[..., 1::2] = words >> 4
        vals = E2M1[nib]
    vals = vals * np.repeat(np.exp2(scales.astype(np.float64) - 127.0), 8, axis=1)[..., None]
    return vals.transpose(0, 1, 3, 2).reshape(g * 512, n)

def pack4(w):
    words, scales = pack_weight(w, "e2m1")
    return words.reshape(words.shape[0], 128, -1), scales


def unpack4(words, scales):
    return unpack_weight(words.reshape(words.shape[0], 128, -1, 2), scales, "e2m1")


N, H, W, K = 512, 2048, 8, 512
TAU = 1.0


def silu(v):
    return v / (1.0 + np.exp(-v))


def softmax_last(v):
    e = np.exp(v - v.max(-1, keepdims=True))
    return e / e.sum(-1, keepdims=True)


def setup_inputs():
    s = np.tile(mx_kscale(K), W)
    x = bf(np.random.standard_normal((N, W * K)) * s)
    t = np.random.standard_normal((H, W * K)) / np.sqrt(K) / s
    words, scales = pack4(np.ascontiguousarray(t.T))
    return {"x": x, "template_flat_words": words, "template_flat_scales": scales}


def reference(x, template_flat_words, template_flat_scales):
    n = x.shape[0]
    xw = f64(x).reshape(n, W, K)
    xq = mxq(xw, 2, "e4m3")
    tq = unpack4(template_flat_words, template_flat_scales).reshape(W, K, -1)
    s = (xq.transpose(1, 0, 2) @ tq).transpose(1, 2, 0)
    gate = softmax_last(s / TAU)
    return np.sum(gate * silu(s), axis=-1)

@@ -1,0 +1,233 @@
+from contextlib import ExitStack
+
+import concourse.masks as masks
+import concourse.mybir as mybir
+
+F32 = mybir.dt.float32
+BF16 = mybir.dt.bfloat16
+I32 = mybir.dt.int32
+U32 = mybir.dt.uint32
+U8 = mybir.dt.uint8
+FP8X4 = mybir.dt.float8_e4m3fn_x4
+FP4X4 = mybir.dt.float4_e2m1fn_x4
+ACT = mybir.ActivationFunctionType
+ALU = mybir.AluOpType
+
+P = 128
+ROWS = 512
+ROW_TILES = ROWS // P
+FEATURES = 2048
+WINDOWS = 8
+K_WINDOW = 512
+BLOCKS = FEATURES // P
+PHASE_BLOCKS = 4
+PHASES = BLOCKS // PHASE_BLOCKS
+PHASE_FEATURES = PHASE_BLOCKS * P
+
+SLOT_PASSES = 4
+HALF = WINDOWS // 2
+SLOTS_HALF_PHASE = PHASE_BLOCKS * WINDOWS // SLOT_PASSES
+SLOTS_PHASE = 2 * SLOTS_HALF_PHASE
+CHUNKS = 4
+SUM_LAG = 13
+
+FLOPS = 2 * ROWS * FEATURES * WINDOWS * K_WINDOW
+
+
+def tile_dendriticlayersilu_ffn_kernel(
+    tc, x, template_flat_words, template_flat_scales, out
+):
+    nc = tc.nc
+    x_by_window = x.rearrange("(t p) (w k) -> w p t k", p=P, k=K_WINDOW)
+    words_by_partition = template_flat_words.rearrange("g p b -> p g b")
+    scales_by_row = template_flat_scales.rearrange("g r h -> r g h")
+    out_by_tile = out.rearrange("(t p) h -> p t h", p=P)
+
+    with ExitStack() as ctx:
+        keep = ctx.enter_context(tc.tile_pool(name="keep", bufs=1))
+        stage = ctx.enter_context(tc.tile_pool(name="stage", bufs=2))
+        work = ctx.enter_context(tc.tile_pool(name="work", bufs=2))
+        banks = ctx.enter_context(tc.psum_pool(name="banks", bufs=6))
+        sums = ctx.enter_context(tc.psum_pool(name="sums", bufs=1))
+
+        ident = keep.tile([P, P], F32, name="ident")
+        xq_codes = keep.tile([P, WINDOWS, ROWS], U32, name="xq_codes", align_bytes=64)
+        xq_scales = keep.tile([P, WINDOWS, ROWS], U8, name="xq_scales", align_bytes=64)
+        w_words = [
+            keep.tile([P, WINDOWS, 2 * PHASE_FEATURES], U8, name="w_words%d" % i, align_bytes=64)
+            for i in range(2)
+        ]
+        w_planes = [
+            keep.tile([P, WINDOWS, PHASE_FEATURES], U8, name="w_planes%d" % i, align_bytes=64)
+            for i in range(2)
+        ]
+        raw = {}
+        peak = {}
+        silu = {}
+        weight = {}
+        den = {}
+        num = {}
+        inv = {}
+
+        def load_window(w):
+            x_raw = stage.tile([P, ROW_TILES, K_WINDOW], BF16, name="x_raw", bufs=3)
+            nc.sync.dma_start(out=x_raw[:], in_=x_by_window[w])
+            raw[w] = x_raw
+
+        def load_weights(phase):
+            cols = slice(PHASE_FEATURES * phase, PHASE_FEATURES * (phase + 1))
+            byte_cols = slice(2 * PHASE_FEATURES * phase, 2 * PHASE_FEATURES * (phase + 1))
+            for quadrant in range(4):
+                nc.sync.dma_start(
+                    out=w_planes[phase % 2][32 * quadrant : 32 * quadrant + 4, :, :].bitcast(I32),
+                    in_=scales_by_row[4 * quadrant : 4 * quadrant + 4, :, cols].bitcast(I32),
+                )
+            nc.sync.dma_start(
+                out=w_words[phase % 2][:].bitcast(I32),
+                in_=words_by_partition[:, :, byte_cols].bitcast(I32),
+            )
+
+        def quantise_window(w):
+            grouped = stage.tile([P, 4 * ROWS], BF16, name="grouped", align_bytes=64)
+            grouped_words = grouped[:].bitcast(F32)
+            for pair in range(2):
+                xt = banks.tile([P, 2, 2 * P], F32, name="xt", tag="bank")
+                for u in range(2):
+                    for i in range(2):
+                        words = raw[w][:, 2 * pair + i, :].bitcast(F32)
+                        nc.tensor.transpose(
+                            xt[:, u, P * i : P * (i + 1)], words[:, u : K_WINDOW // 2 : 2], ident[:]
+                        )
+                nc.scalar.copy(
+                    out=grouped_words[:, 4 * P * pair : 4 * P * (pair + 1)].rearrange(
+                        "p (n u) -> p n u", u=2
+                    ),
+                    in_=xt[:].rearrange("p u n -> p n u"),
+                )
+            nc.vector.quantize_mx(
+                out=xq_codes[:, w, :].bitcast(FP8X4), scales=xq_scales[:, w, :], in_=grouped[:]
+            )
+            if w + 3 < WINDOWS:
+                load_window(w + 3)
+
+        def score_pass(block, w):
+            phase, j = divmod(block, PHASE_BLOCKS)
+            bank = banks.tile([P, ROWS], F32, name="bank", tag="bank")
+            nc.tensor.matmul_mx(
+                out=bank[:],
+                lhsT=w_words[phase % 2][:, w, 2 * P * j : 2 * P * (j + 1)].bitcast(FP4X4),
+                lhsT_scale=w_planes[phase % 2][:, w, P * j : P * (j + 1)],
+                rhs=xq_codes[:, w, :].bitcast(FP8X4),
+                rhs_scale=xq_scales[:, w, :],
+                start=True,
+                stop=True,
+            )
+            return bank
+
+        def peak_and_silu(block, w):
+            if w == 0:
+                peak_tile = work.tile([P, ROWS], F32, name="peak", bufs=4)
+                peak[block] = peak_tile
+                silu_tile = work.tile([P, WINDOWS, ROWS], F32, name="silu", bufs=6)
+                silu[block] = silu_tile
+            bank = score_pass(block, w)
+            if w == 0:
+                nc.vector.tensor_copy(out=peak[block][:], in_=bank[:])
+            else:
+                nc.vector.tensor_tensor(
+                    out=peak[block][:], in0=peak[block][:], in1=bank[:], op=ALU.max
+                )
+            nc.scalar.activation(out=silu[block][:, w, :], in_=bank[:], func=ACT.Silu)
+
+        def softmax_weight(block, w):
+            if w == 0:
+                weight_tile = work.tile([P, WINDOWS, ROWS], F32, name="weight", bufs=3)
+                weight[block] = weight_tile
+            bank = score_pass(block, w)
+            nc.vector.tensor_tensor(
+                out=weight[block][:, w, :], in0=bank[:], in1=peak[block][:], op=ALU.subtract
+            )
+            nc.scalar.activation(
+                out=weight[block][:, w, :], in_=weight[block][:, w, :], func=ACT.Exp
+            )
+
+        def multiply(block, half):
+            ws = slice(HALF * half, HALF * (half + 1))
+            nc.gpsimd.tensor_tensor(
+                out=silu[block][:, ws, :],
+                in0=silu[block][:, ws, :],
+                in1=weight[block][:, ws, :],
+                op=ALU.mult,
+            )
+
+        def add_windows(total, terms, t):
+            for w in range(WINDOWS):
+                nc.tensor.matmul(
+                    out=total[:, t, :],
+                    lhsT=terms[:, w, P * t : P * (t + 1)],
+                    rhs=ident[:],
+                    is_transpose=True,
+                    start=(w == 0),
+                    stop=(w == WINDOWS - 1),
+                )
+
+        def add_chunk(block, chunk):
+            if chunk == 0:
+                den_bank = sums.tile([P, ROW_TILES, P], F32, name="den")
+                den[block] = den_bank
+            if chunk == 2:
+                num_bank = sums.tile([P, ROW_TILES, P], F32, name="num")
+                num[block] = num_bank
+            for t in range(2 * (chunk % 2), 2 * (chunk % 2) + 2):
+                if chunk < 2:
+                    add_windows(den[block], weight[block], t)
+                else:
+                    add_windows(num[block], silu[block], t)
+
+        def invert(block):
+            inv_tile = work.tile([P, ROW_TILES, P], F32, name="inv")
+            inv[block] = inv_tile
+            nc.vector.reciprocal(out=inv_tile[:], in_=den[block][:])
+
+        def finish(block):
+            result = work.tile([P, ROW_TILES, P], F32, name="result", bufs=3)
+            nc.vector.tensor_tensor(out=result[:], in0=num[block][:], in1=inv[block][:], op=ALU.mult)
+            nc.sync.dma_start(out=out_by_tile[:, :, P * block : P * (block + 1)], in_=result[:])
+
+        with tc.manual_schedule():
+            for plane in w_planes:
+                nc.vector.memset(plane[:].bitcast(I32), 0)
+            masks.make_identity(nc, ident[:])
+            load_window(0)
+            load_window(1)
+            load_weights(0)
+            load_window(2)
+            quantise_window(0)
+
+            for slot in range(PHASES * SLOTS_PHASE + SUM_LAG + 1):
+                phase, pos = divmod(slot, SLOTS_PHASE)
+                first = PHASE_BLOCKS * phase
+                half = pos % 2
+                if phase == 0 and pos < SLOTS_HALF_PHASE:
+                    if pos + 1 < WINDOWS:
+                        quantise_window(pos + 1)
+                    for j in range(PHASE_BLOCKS):
+                        peak_and_silu(first + j, pos)
+                elif phase < PHASES and pos < SLOTS_HALF_PHASE:
+                    for w in range(HALF * half, HALF * (half + 1)):
+                        peak_and_silu(first + pos // 2, w)
+                elif phase < PHASES:
+                    if pos == SLOTS_HALF_PHASE and phase + 1 < PHASES:
+                        load_weights(phase + 1)
+                    block = first + (pos - SLOTS_HALF_PHASE) // 2
+                    for w in range(HALF * half, HALF * (half + 1)):
+                        softmax_weight(block, w)
+                    multiply(block, half)
+
+                lagged = slot - SUM_LAG
+                if 0 <= lagged < BLOCKS * CHUNKS:
+                    add_chunk(lagged // CHUNKS, lagged % CHUNKS)
+                    if lagged % CHUNKS == 2:
+                        invert(lagged // CHUNKS)
+                if lagged >= CHUNKS and lagged % CHUNKS == 0:
+                    finish(lagged // CHUNKS - 1)

@@ -160,16 +160,17 @@ def tile_dendriticlayersilu_ffn_kernel(
                 op=ALU.mult,
             )
 
-        def add_windows(total, terms, t):
-            for w in range(WINDOWS):
-                nc.tensor.matmul(
-                    out=total[:, t, :],
-                    lhsT=terms[:, w, P * t : P * (t + 1)],
-                    rhs=ident[:],
-                    is_transpose=True,
-                    start=(w == 0),
-                    stop=(w == WINDOWS - 1),
-                )
+        def add_windows(total, terms, half):
+            for w in range(HALF * half, HALF * (half + 1)):
+                for t in range(ROW_TILES):
+                    nc.tensor.matmul(
+                        out=total[:, t, :],
+                        lhsT=terms[:, w, P * t : P * (t + 1)],
+                        rhs=ident[:],
+                        is_transpose=True,
+                        start=(w == 0 and t == 0),
+                        stop=(w == WINDOWS - 1 and t == ROW_TILES - 1),
+                    )
 
         def add_chunk(block, chunk):
             if chunk == 0:
@@ -178,11 +179,10 @@ def tile_dendriticlayersilu_ffn_kernel(
             if chunk == 2:
                 num_bank = sums.tile([P, ROW_TILES, P], F32, name="num")
                 num[block] = num_bank
-            for t in range(2 * (chunk % 2), 2 * (chunk % 2) + 2):
-                if chunk < 2:
-                    add_windows(den[block], weight[block], t)
-                else:
-                    add_windows(num[block], silu[block], t)
+            if chunk < 2:
+                add_windows(den[block], weight[block], chunk % 2)
+            else:
+                add_windows(num[block], silu[block], chunk % 2)
 
         def invert(block):
             inv_tile = work.tile([P, ROW_TILES, P], F32, name="inv")

@@ -18,18 +18,15 @@ ROWS = 512
 ROW_TILES = ROWS // P
 FEATURES = 2048
 WINDOWS = 8
+HALF = WINDOWS // 2
 K_WINDOW = 512
 BLOCKS = FEATURES // P
-PHASE_BLOCKS = 4
-PHASES = BLOCKS // PHASE_BLOCKS
-PHASE_FEATURES = PHASE_BLOCKS * P
+PHASE_SIZES = (4, 4, 4, 4)
+MAX_PHASE = max(PHASE_SIZES)
+CHAINS = 2
 
 SLOT_PASSES = 4
-HALF = WINDOWS // 2
-SLOTS_HALF_PHASE = PHASE_BLOCKS * WINDOWS // SLOT_PASSES
-SLOTS_PHASE = 2 * SLOTS_HALF_PHASE
-CHUNKS = 4
-SUM_LAG = 13
+ADD_LAG = 44
 
 FLOPS = 2 * ROWS * FEATURES * WINDOWS * K_WINDOW
 
@@ -43,6 +40,32 @@ def tile_dendriticlayersilu_ffn_kernel(
     scales_by_row = template_flat_scales.rearrange("g r h -> r g h")
     out_by_tile = out.rearrange("(t p) h -> p t h", p=P)
 
+    phases = []
+    for size in PHASE_SIZES:
+        first = sum(len(blocks) for blocks in phases)
+        phases.append(list(range(first, first + size)))
+    assert sum(PHASE_SIZES) == BLOCKS
+    phase_of = {}
+    for index, blocks in enumerate(phases):
+        for block in blocks:
+            phase_of[block] = index
+
+    passes = []
+    for index, blocks in enumerate(phases):
+        group = len(blocks) if index == 0 else CHAINS
+        for first in range(0, len(blocks), group):
+            passes.extend(
+                ("peak", block, w) for w in range(WINDOWS) for block in blocks[first : first + group]
+            )
+        passes.extend(("weight", block, w) for block in blocks for w in range(WINDOWS))
+    additions = [
+        (block, kind, w)
+        for block in range(BLOCKS)
+        for kind in ("weight", "product")
+        for w in range(WINDOWS)
+    ]
+    assert len(additions) == len(passes)
+
     with ExitStack() as ctx:
         keep = ctx.enter_context(tc.tile_pool(name="keep", bufs=1))
         stage = ctx.enter_context(tc.tile_pool(name="stage", bufs=2))
@@ -54,19 +77,18 @@ def tile_dendriticlayersilu_ffn_kernel(
         xq_codes = keep.tile([P, WINDOWS, ROWS], U32, name="xq_codes", align_bytes=64)
         xq_scales = keep.tile([P, WINDOWS, ROWS], U8, name="xq_scales", align_bytes=64)
         w_words = [
-            keep.tile([P, WINDOWS, 2 * PHASE_FEATURES], U8, name="w_words%d" % i, align_bytes=64)
+            keep.tile([P, WINDOWS, 2 * P * MAX_PHASE], U8, name="w_words%d" % i, align_bytes=64)
             for i in range(2)
         ]
         w_planes = [
-            keep.tile([P, WINDOWS, PHASE_FEATURES], U8, name="w_planes%d" % i, align_bytes=64)
+            keep.tile([P, WINDOWS, P * MAX_PHASE], U8, name="w_planes%d" % i, align_bytes=64)
             for i in range(2)
         ]
         raw = {}
         peak = {}
         silu = {}
         weight = {}
-        den = {}
-        num = {}
+        total = {}
         inv = {}
 
         def load_window(w):
@@ -74,16 +96,18 @@ def tile_dendriticlayersilu_ffn_kernel(
             nc.sync.dma_start(out=x_raw[:], in_=x_by_window[w])
             raw[w] = x_raw
 
-        def load_weights(phase):
-            cols = slice(PHASE_FEATURES * phase, PHASE_FEATURES * (phase + 1))
-            byte_cols = slice(2 * PHASE_FEATURES * phase, 2 * PHASE_FEATURES * (phase + 1))
+        def load_weights(index):
+            blocks = phases[index]
+            width = P * len(blocks)
+            cols = slice(P * blocks[0], P * blocks[0] + width)
+            byte_cols = slice(2 * P * blocks[0], 2 * (P * blocks[0] + width))
             for quadrant in range(4):
                 nc.sync.dma_start(
-                    out=w_planes[phase % 2][32 * quadrant : 32 * quadrant + 4, :, :].bitcast(I32),
+                    out=w_planes[index % 2][32 * quadrant : 32 * quadrant + 4, :, :width].bitcast(I32),
                     in_=scales_by_row[4 * quadrant : 4 * quadrant + 4, :, cols].bitcast(I32),
                 )
             nc.sync.dma_start(
-                out=w_words[phase % 2][:].bitcast(I32),
+                out=w_words[index % 2][:, :, : 2 * width].bitcast(I32),
                 in_=words_by_partition[:, :, byte_cols].bitcast(I32),
             )
 
@@ -111,12 +135,13 @@ def tile_dendriticlayersilu_ffn_kernel(
                 load_window(w + 3)
 
         def score_pass(block, w):
-            phase, j = divmod(block, PHASE_BLOCKS)
+            index = phase_of[block]
+            j = block - phases[index][0]
             bank = banks.tile([P, ROWS], F32, name="bank", tag="bank")
             nc.tensor.matmul_mx(
                 out=bank[:],
-                lhsT=w_words[phase % 2][:, w, 2 * P * j : 2 * P * (j + 1)].bitcast(FP4X4),
-                lhsT_scale=w_planes[phase % 2][:, w, P * j : P * (j + 1)],
+                lhsT=w_words[index % 2][:, w, 2 * P * j : 2 * P * (j + 1)].bitcast(FP4X4),
+                lhsT_scale=w_planes[index % 2][:, w, P * j : P * (j + 1)],
                 rhs=xq_codes[:, w, :].bitcast(FP8X4),
                 rhs_scale=xq_scales[:, w, :],
                 start=True,
@@ -126,7 +151,7 @@ def tile_dendriticlayersilu_ffn_kernel(
 
         def peak_and_silu(block, w):
             if w == 0:
-                peak_tile = work.tile([P, ROWS], F32, name="peak", bufs=4)
+                peak_tile = work.tile([P, ROWS], F32, name="peak", bufs=MAX_PHASE)
                 peak[block] = peak_tile
                 silu_tile = work.tile([P, WINDOWS, ROWS], F32, name="silu", bufs=6)
                 silu[block] = silu_tile
@@ -151,47 +176,40 @@ def tile_dendriticlayersilu_ffn_kernel(
                 out=weight[block][:, w, :], in_=weight[block][:, w, :], func=ACT.Exp
             )
 
-        def multiply(block, half):
+        def multiply(engine, block, half):
             ws = slice(HALF * half, HALF * (half + 1))
-            nc.gpsimd.tensor_tensor(
+            engine.tensor_tensor(
                 out=silu[block][:, ws, :],
                 in0=silu[block][:, ws, :],
                 in1=weight[block][:, ws, :],
                 op=ALU.mult,
             )
 
-        def add_windows(total, terms, half):
-            for w in range(HALF * half, HALF * (half + 1)):
-                for t in range(ROW_TILES):
-                    nc.tensor.matmul(
-                        out=total[:, t, :],
-                        lhsT=terms[:, w, P * t : P * (t + 1)],
-                        rhs=ident[:],
-                        is_transpose=True,
-                        start=(w == 0 and t == 0),
-                        stop=(w == WINDOWS - 1 and t == ROW_TILES - 1),
-                    )
-
-        def add_chunk(block, chunk):
-            if chunk == 0:
-                den_bank = sums.tile([P, ROW_TILES, P], F32, name="den")
-                den[block] = den_bank
-            if chunk == 2:
-                num_bank = sums.tile([P, ROW_TILES, P], F32, name="num")
-                num[block] = num_bank
-            if chunk < 2:
-                add_windows(den[block], weight[block], chunk % 2)
-            else:
-                add_windows(num[block], silu[block], chunk % 2)
+        def add_window(block, kind, w):
+            if w == 0:
+                bank = sums.tile([P, ROW_TILES, P], F32, name=kind + "_sum")
+                total[kind, block] = bank
+            terms = weight[block] if kind == "weight" else silu[block]
+            for t in range(ROW_TILES):
+                nc.tensor.matmul(
+                    out=total[kind, block][:, t, :],
+                    lhsT=terms[:, w, P * t : P * (t + 1)],
+                    rhs=ident[:],
+                    is_transpose=True,
+                    start=(w == 0 and t == 0),
+                    stop=(w == WINDOWS - 1 and t == ROW_TILES - 1),
+                )
 
         def invert(block):
             inv_tile = work.tile([P, ROW_TILES, P], F32, name="inv")
             inv[block] = inv_tile
-            nc.vector.reciprocal(out=inv_tile[:], in_=den[block][:])
+            nc.vector.reciprocal(out=inv_tile[:], in_=total["weight", block][:])
 
         def finish(block):
             result = work.tile([P, ROW_TILES, P], F32, name="result", bufs=3)
-            nc.vector.tensor_tensor(out=result[:], in0=num[block][:], in1=inv[block][:], op=ALU.mult)
+            nc.vector.tensor_tensor(
+                out=result[:], in0=total["product", block][:], in1=inv[block][:], op=ALU.mult
+            )
             nc.sync.dma_start(out=out_by_tile[:, :, P * block : P * (block + 1)], in_=result[:])
 
         with tc.manual_schedule():
@@ -204,30 +222,27 @@ def tile_dendriticlayersilu_ffn_kernel(
             load_window(2)
             quantise_window(0)
 
-            for slot in range(PHASES * SLOTS_PHASE + SUM_LAG + 1):
-                phase, pos = divmod(slot, SLOTS_PHASE)
-                first = PHASE_BLOCKS * phase
-                half = pos % 2
-                if phase == 0 and pos < SLOTS_HALF_PHASE:
-                    if pos + 1 < WINDOWS:
-                        quantise_window(pos + 1)
-                    for j in range(PHASE_BLOCKS):
-                        peak_and_silu(first + j, pos)
-                elif phase < PHASES and pos < SLOTS_HALF_PHASE:
-                    for w in range(HALF * half, HALF * (half + 1)):
-                        peak_and_silu(first + pos // 2, w)
-                elif phase < PHASES:
-                    if pos == SLOTS_HALF_PHASE and phase + 1 < PHASES:
-                        load_weights(phase + 1)
-                    block = first + (pos - SLOTS_HALF_PHASE) // 2
-                    for w in range(HALF * half, HALF * (half + 1)):
+            closed = []
+            for start in range(0, len(passes) + ADD_LAG + SLOT_PASSES, SLOT_PASSES):
+                for kind, block, w in passes[start : start + SLOT_PASSES]:
+                    if kind == "peak":
+                        if block == 0 and w + 1 < WINDOWS:
+                            quantise_window(w + 1)
+                        peak_and_silu(block, w)
+                    else:
+                        index = phase_of[block]
+                        if block == phases[index][0] and w == 0 and index + 1 < len(phases):
+                            load_weights(index + 1)
                         softmax_weight(block, w)
-                    multiply(block, half)
-
-                lagged = slot - SUM_LAG
-                if 0 <= lagged < BLOCKS * CHUNKS:
-                    add_chunk(lagged // CHUNKS, lagged % CHUNKS)
-                    if lagged % CHUNKS == 2:
-                        invert(lagged // CHUNKS)
-                if lagged >= CHUNKS and lagged % CHUNKS == 0:
-                    finish(lagged // CHUNKS - 1)
+                        if w % HALF == HALF - 1:
+                            multiply(nc.gpsimd, block, w // HALF)
+                for block, kind in closed:
+                    if kind == "weight":
+                        invert(block)
+                    else:
+                        finish(block)
+                closed = []
+                for block, kind, w in additions[max(start - ADD_LAG, 0) : max(start - ADD_LAG + SLOT_PASSES, 0)]:
+                    add_window(block, kind, w)
+                    if w == WINDOWS - 1:
+                        closed.append((block, kind))

@@ -21,12 +21,12 @@ WINDOWS = 8
 HALF = WINDOWS // 2
 K_WINDOW = 512
 BLOCKS = FEATURES // P
-PHASE_SIZES = (4, 4, 4, 4)
-MAX_PHASE = max(PHASE_SIZES)
-CHAINS = 2
+PHASE_BLOCKS = 2
+PHASES = BLOCKS // PHASE_BLOCKS
+PHASE_FEATURES = PHASE_BLOCKS * P
 
 SLOT_PASSES = 4
-ADD_LAG = 44
+ADD_LAG = 24
 
 FLOPS = 2 * ROWS * FEATURES * WINDOWS * K_WINDOW
 
@@ -40,23 +40,10 @@ def tile_dendriticlayersilu_ffn_kernel(
     scales_by_row = template_flat_scales.rearrange("g r h -> r g h")
     out_by_tile = out.rearrange("(t p) h -> p t h", p=P)
 
-    phases = []
-    for size in PHASE_SIZES:
-        first = sum(len(blocks) for blocks in phases)
-        phases.append(list(range(first, first + size)))
-    assert sum(PHASE_SIZES) == BLOCKS
-    phase_of = {}
-    for index, blocks in enumerate(phases):
-        for block in blocks:
-            phase_of[block] = index
-
     passes = []
-    for index, blocks in enumerate(phases):
-        group = len(blocks) if index == 0 else CHAINS
-        for first in range(0, len(blocks), group):
-            passes.extend(
-                ("peak", block, w) for w in range(WINDOWS) for block in blocks[first : first + group]
-            )
+    for phase in range(PHASES):
+        blocks = range(PHASE_BLOCKS * phase, PHASE_BLOCKS * (phase + 1))
+        passes.extend(("peak", block, w) for w in range(WINDOWS) for block in blocks)
         passes.extend(("weight", block, w) for block in blocks for w in range(WINDOWS))
     additions = [
         (block, kind, w)
@@ -64,7 +51,6 @@ def tile_dendriticlayersilu_ffn_kernel(
         for kind in ("weight", "product")
         for w in range(WINDOWS)
     ]
-    assert len(additions) == len(passes)
 
     with ExitStack() as ctx:
         keep = ctx.enter_context(tc.tile_pool(name="keep", bufs=1))
@@ -74,14 +60,15 @@ def tile_dendriticlayersilu_ffn_kernel(
         sums = ctx.enter_context(tc.psum_pool(name="sums", bufs=1))
 
         ident = keep.tile([P, P], F32, name="ident")
+        warm = keep.tile([P, 1], F32, name="warm")
         xq_codes = keep.tile([P, WINDOWS, ROWS], U32, name="xq_codes", align_bytes=64)
         xq_scales = keep.tile([P, WINDOWS, ROWS], U8, name="xq_scales", align_bytes=64)
         w_words = [
-            keep.tile([P, WINDOWS, 2 * P * MAX_PHASE], U8, name="w_words%d" % i, align_bytes=64)
+            keep.tile([P, WINDOWS, 2 * PHASE_FEATURES], U8, name="w_words%d" % i, align_bytes=64)
             for i in range(2)
         ]
-        w_planes = [
-            keep.tile([P, WINDOWS, P * MAX_PHASE], U8, name="w_planes%d" % i, align_bytes=64)
+        w_scales = [
+            keep.tile([P, WINDOWS, PHASE_FEATURES], U8, name="w_scales%d" % i, align_bytes=64)
             for i in range(2)
         ]
         raw = {}
@@ -89,25 +76,23 @@ def tile_dendriticlayersilu_ffn_kernel(
         silu = {}
         weight = {}
         total = {}
-        inv = {}
+        inverse = {}
 
         def load_window(w):
             x_raw = stage.tile([P, ROW_TILES, K_WINDOW], BF16, name="x_raw", bufs=3)
             nc.sync.dma_start(out=x_raw[:], in_=x_by_window[w])
             raw[w] = x_raw
 
-        def load_weights(index):
-            blocks = phases[index]
-            width = P * len(blocks)
-            cols = slice(P * blocks[0], P * blocks[0] + width)
-            byte_cols = slice(2 * P * blocks[0], 2 * (P * blocks[0] + width))
+        def load_weights(phase):
+            cols = slice(PHASE_FEATURES * phase, PHASE_FEATURES * (phase + 1))
+            byte_cols = slice(2 * PHASE_FEATURES * phase, 2 * PHASE_FEATURES * (phase + 1))
             for quadrant in range(4):
                 nc.sync.dma_start(
-                    out=w_planes[index % 2][32 * quadrant : 32 * quadrant + 4, :, :width].bitcast(I32),
+                    out=w_scales[phase % 2][32 * quadrant : 32 * quadrant + 4, :, :].bitcast(I32),
                     in_=scales_by_row[4 * quadrant : 4 * quadrant + 4, :, cols].bitcast(I32),
                 )
             nc.sync.dma_start(
-                out=w_words[index % 2][:, :, : 2 * width].bitcast(I32),
+                out=w_words[phase % 2][:].bitcast(I32),
                 in_=words_by_partition[:, :, byte_cols].bitcast(I32),
             )
 
@@ -122,12 +107,13 @@ def tile_dendriticlayersilu_ffn_kernel(
                         nc.tensor.transpose(
                             xt[:, u, P * i : P * (i + 1)], words[:, u : K_WINDOW // 2 : 2], ident[:]
                         )
-                nc.scalar.copy(
-                    out=grouped_words[:, 4 * P * pair : 4 * P * (pair + 1)].rearrange(
-                        "p (n u) -> p n u", u=2
-                    ),
-                    in_=xt[:].rearrange("p u n -> p n u"),
+                side_by_side = grouped_words[:, 4 * P * pair : 4 * P * (pair + 1)].rearrange(
+                    "p (n u) -> p n u", u=2
                 )
+                if pair == 0:
+                    nc.scalar.copy(out=side_by_side, in_=xt[:].rearrange("p u n -> p n u"))
+                else:
+                    nc.vector.tensor_copy(out=side_by_side, in_=xt[:].rearrange("p u n -> p n u"))
             nc.vector.quantize_mx(
                 out=xq_codes[:, w, :].bitcast(FP8X4), scales=xq_scales[:, w, :], in_=grouped[:]
             )
@@ -135,13 +121,12 @@ def tile_dendriticlayersilu_ffn_kernel(
                 load_window(w + 3)
 
         def score_pass(block, w):
-            index = phase_of[block]
-            j = block - phases[index][0]
+            phase, place = divmod(block, PHASE_BLOCKS)
             bank = banks.tile([P, ROWS], F32, name="bank", tag="bank")
             nc.tensor.matmul_mx(
                 out=bank[:],
-                lhsT=w_words[index % 2][:, w, 2 * P * j : 2 * P * (j + 1)].bitcast(FP4X4),
-                lhsT_scale=w_planes[index % 2][:, w, P * j : P * (j + 1)],
+                lhsT=w_words[phase % 2][:, w, 2 * P * place : 2 * P * (place + 1)].bitcast(FP4X4),
+                lhsT_scale=w_scales[phase % 2][:, w, P * place : P * (place + 1)],
                 rhs=xq_codes[:, w, :].bitcast(FP8X4),
                 rhs_scale=xq_scales[:, w, :],
                 start=True,
@@ -151,7 +136,7 @@ def tile_dendriticlayersilu_ffn_kernel(
 
         def peak_and_silu(block, w):
             if w == 0:
-                peak_tile = work.tile([P, ROWS], F32, name="peak", bufs=MAX_PHASE)
+                peak_tile = work.tile([P, ROWS], F32, name="peak", bufs=PHASE_BLOCKS)
                 peak[block] = peak_tile
                 silu_tile = work.tile([P, WINDOWS, ROWS], F32, name="silu", bufs=6)
                 silu[block] = silu_tile
@@ -176,9 +161,9 @@ def tile_dendriticlayersilu_ffn_kernel(
                 out=weight[block][:, w, :], in_=weight[block][:, w, :], func=ACT.Exp
             )
 
-        def multiply(engine, block, half):
+        def multiply(block, half):
             ws = slice(HALF * half, HALF * (half + 1))
-            engine.tensor_tensor(
+            nc.gpsimd.tensor_tensor(
                 out=silu[block][:, ws, :],
                 in0=silu[block][:, ws, :],
                 in1=weight[block][:, ws, :],
@@ -201,48 +186,49 @@ def tile_dendriticlayersilu_ffn_kernel(
                 )
 
         def invert(block):
-            inv_tile = work.tile([P, ROW_TILES, P], F32, name="inv")
-            inv[block] = inv_tile
-            nc.vector.reciprocal(out=inv_tile[:], in_=total["weight", block][:])
+            inverse_tile = work.tile([P, ROW_TILES, P], F32, name="inverse")
+            inverse[block] = inverse_tile
+            nc.vector.reciprocal(out=inverse_tile[:], in_=total["weight", block][:])
 
         def finish(block):
             result = work.tile([P, ROW_TILES, P], F32, name="result", bufs=3)
             nc.vector.tensor_tensor(
-                out=result[:], in0=total["product", block][:], in1=inv[block][:], op=ALU.mult
+                out=result[:], in0=total["product", block][:], in1=inverse[block][:], op=ALU.mult
             )
             nc.sync.dma_start(out=out_by_tile[:, :, P * block : P * (block + 1)], in_=result[:])
 
-        with tc.manual_schedule():
-            for plane in w_planes:
-                nc.vector.memset(plane[:].bitcast(I32), 0)
-            masks.make_identity(nc, ident[:])
-            load_window(0)
-            load_window(1)
-            load_weights(0)
-            load_window(2)
-            quantise_window(0)
+        for scales in w_scales:
+            nc.vector.memset(scales[:].bitcast(I32), 0)
+        masks.make_identity(nc, ident[:])
+        nc.vector.memset(warm[:], 0.0)
+        nc.scalar.activation(out=warm[:], in_=warm[:], func=ACT.Silu)
+        load_window(0)
+        load_window(1)
+        load_weights(0)
+        load_window(2)
+        quantise_window(0)
 
+        closed = []
+        for start in range(0, len(passes) + ADD_LAG + SLOT_PASSES, SLOT_PASSES):
+            for kind, block, w in passes[start : start + SLOT_PASSES]:
+                if kind == "peak":
+                    if block == 0 and w + 1 < WINDOWS:
+                        quantise_window(w + 1)
+                    peak_and_silu(block, w)
+                else:
+                    phase, place = divmod(block, PHASE_BLOCKS)
+                    if place == 0 and w == 0 and phase + 1 < PHASES:
+                        load_weights(phase + 1)
+                    softmax_weight(block, w)
+                    if w % HALF == HALF - 1:
+                        multiply(block, w // HALF)
+            for block, kind in closed:
+                if kind == "weight":
+                    invert(block)
+                else:
+                    finish(block)
             closed = []
-            for start in range(0, len(passes) + ADD_LAG + SLOT_PASSES, SLOT_PASSES):
-                for kind, block, w in passes[start : start + SLOT_PASSES]:
-                    if kind == "peak":
-                        if block == 0 and w + 1 < WINDOWS:
-                            quantise_window(w + 1)
-                        peak_and_silu(block, w)
-                    else:
-                        index = phase_of[block]
-                        if block == phases[index][0] and w == 0 and index + 1 < len(phases):
-                            load_weights(index + 1)
-                        softmax_weight(block, w)
-                        if w % HALF == HALF - 1:
-                            multiply(nc.gpsimd, block, w // HALF)
-                for block, kind in closed:
-                    if kind == "weight":
-                        invert(block)
-                    else:
-                        finish(block)
-                closed = []
-                for block, kind, w in additions[max(start - ADD_LAG, 0) : max(start - ADD_LAG + SLOT_PASSES, 0)]:
-                    add_window(block, kind, w)
-                    if w == WINDOWS - 1:
-                        closed.append((block, kind))
+            for block, kind, w in additions[max(start - ADD_LAG, 0) : max(start - ADD_LAG + SLOT_PASSES, 0)]:
+                add_window(block, kind, w)
+                if w == WINDOWS - 1:
+                    closed.append((block, kind))

@@ -186,15 +186,14 @@ def tile_dendriticlayersilu_ffn_kernel(
                 )
 
         def invert(block):
-            inverse_tile = work.tile([P, ROW_TILES, P], F32, name="inverse")
+            inverse_tile = work.tile([P, ROW_TILES, P], F32, name="inverse", bufs=3)
             inverse[block] = inverse_tile
             nc.vector.reciprocal(out=inverse_tile[:], in_=total["weight", block][:])
 
         def finish(block):
             result = work.tile([P, ROW_TILES, P], F32, name="result", bufs=3)
-            nc.vector.tensor_tensor(
-                out=result[:], in0=total["product", block][:], in1=inverse[block][:], op=ALU.mult
-            )
+            nc.scalar.copy(out=result[:], in_=total["product", block][:])
+            nc.gpsimd.tensor_tensor(out=result[:], in0=result[:], in1=inverse[block][:], op=ALU.mult)
             nc.sync.dma_start(out=out_by_tile[:, :, P * block : P * (block + 1)], in_=result[:])
 
         for scales in w_scales:

@@ -28,6 +28,10 @@ PHASE_FEATURES = PHASE_BLOCKS * P
 SLOT_PASSES = 4
 ADD_LAG = 24
 
+VECTOR_ENDS = 2
+
+VECTOR_HALVES = 1
+
 FLOPS = 2 * ROWS * FEATURES * WINDOWS * K_WINDOW
 
 
@@ -163,7 +167,9 @@ def tile_dendriticlayersilu_ffn_kernel(
 
         def multiply(block, half):
             ws = slice(HALF * half, HALF * (half + 1))
-            nc.gpsimd.tensor_tensor(
+            late = 2 * (BLOCKS - 1 - block) + (1 - half) < VECTOR_HALVES
+            engine = nc.vector if late else nc.gpsimd
+            engine.tensor_tensor(
                 out=silu[block][:, ws, :],
                 in0=silu[block][:, ws, :],
                 in1=weight[block][:, ws, :],
@@ -192,8 +198,15 @@ def tile_dendriticlayersilu_ffn_kernel(
 
         def finish(block):
             result = work.tile([P, ROW_TILES, P], F32, name="result", bufs=3)
-            nc.scalar.copy(out=result[:], in_=total["product", block][:])
-            nc.gpsimd.tensor_tensor(out=result[:], in0=result[:], in1=inverse[block][:], op=ALU.mult)
+            if block < BLOCKS - VECTOR_ENDS:
+                nc.scalar.copy(out=result[:], in_=total["product", block][:])
+                nc.gpsimd.tensor_tensor(
+                    out=result[:], in0=result[:], in1=inverse[block][:], op=ALU.mult
+                )
+            else:
+                nc.vector.tensor_tensor(
+                    out=result[:], in0=total["product", block][:], in1=inverse[block][:], op=ALU.mult
+                )
             nc.sync.dma_start(out=out_by_tile[:, :, P * block : P * (block + 1)], in_=result[:])
 
         for scales in w_scales:

@@ -60,8 +60,7 @@ def tile_dendriticlayersilu_ffn_kernel(
         keep = ctx.enter_context(tc.tile_pool(name="keep", bufs=1))
         stage = ctx.enter_context(tc.tile_pool(name="stage", bufs=2))
         work = ctx.enter_context(tc.tile_pool(name="work", bufs=2))
-        banks = ctx.enter_context(tc.psum_pool(name="banks", bufs=6))
-        sums = ctx.enter_context(tc.psum_pool(name="sums", bufs=1))
+        banks = ctx.enter_context(tc.psum_pool(name="banks", bufs=8))
 
         ident = keep.tile([P, P], F32, name="ident")
         warm = keep.tile([P, 1], F32, name="warm")
@@ -178,7 +177,7 @@ def tile_dendriticlayersilu_ffn_kernel(
 
         def add_window(block, kind, w):
             if w == 0:
-                bank = sums.tile([P, ROW_TILES, P], F32, name=kind + "_sum")
+                bank = banks.tile([P, ROW_TILES, P], F32, name="window_sum", tag="bank")
                 total[kind, block] = bank
             terms = weight[block] if kind == "weight" else silu[block]
             for t in range(ROW_TILES):

@@ -21,16 +21,21 @@ WINDOWS = 8
 HALF = WINDOWS // 2
 K_WINDOW = 512
 BLOCKS = FEATURES // P
-PHASE_BLOCKS = 2
-PHASES = BLOCKS // PHASE_BLOCKS
-PHASE_FEATURES = PHASE_BLOCKS * P
+PHASE_SIZES = (2, 2, 2, 2, 2, 2, 2, 2)
+MAX_PHASE = max(PHASE_SIZES)
+PHASES = len(PHASE_SIZES)
 
 SLOT_PASSES = 4
 ADD_LAG = 24
-
-VECTOR_ENDS = 2
-
 VECTOR_HALVES = 1
+SILU_BUFS = 6
+WEIGHT_BUFS = 3
+X_BUFS = 3
+PEAK_GROUP = 2
+SCALAR_COPIES = (0, 0, 0, 0, 0, 0, 0, 0)
+FIRST_ON_SCALAR = 0
+V_FINALS = BLOCKS
+TAIL = 1
 
 FLOPS = 2 * ROWS * FEATURES * WINDOWS * K_WINDOW
 
@@ -44,17 +49,26 @@ def tile_dendriticlayersilu_ffn_kernel(
     scales_by_row = template_flat_scales.rearrange("g r h -> r g h")
     out_by_tile = out.rearrange("(t p) h -> p t h", p=P)
 
+    phase_of = []
+    place_of = []
+    first_of = []
+    for phase, size in enumerate(PHASE_SIZES):
+        first_of.append(len(phase_of))
+        for place in range(size):
+            phase_of.append(phase)
+            place_of.append(place)
+
     passes = []
-    for phase in range(PHASES):
-        blocks = range(PHASE_BLOCKS * phase, PHASE_BLOCKS * (phase + 1))
-        passes.extend(("peak", block, w) for w in range(WINDOWS) for block in blocks)
+    for phase, size in enumerate(PHASE_SIZES):
+        blocks = list(range(first_of[phase], first_of[phase] + size))
+        for g in range(0, size, PEAK_GROUP):
+            passes.extend(("peak", block, w) for w in range(WINDOWS) for block in blocks[g : g + PEAK_GROUP])
         passes.extend(("weight", block, w) for block in blocks for w in range(WINDOWS))
-    additions = [
-        (block, kind, w)
-        for block in range(BLOCKS)
-        for kind in ("weight", "product")
-        for w in range(WINDOWS)
-    ]
+    additions = []
+    for pair in range(0, BLOCKS, 2):
+        for kind in ("weight", "product"):
+            for block in (pair, pair + 1):
+                additions.extend((block, kind, w) for w in range(WINDOWS))
 
     with ExitStack() as ctx:
         keep = ctx.enter_context(tc.tile_pool(name="keep", bufs=1))
@@ -67,11 +81,11 @@ def tile_dendriticlayersilu_ffn_kernel(
         xq_codes = keep.tile([P, WINDOWS, ROWS], U32, name="xq_codes", align_bytes=64)
         xq_scales = keep.tile([P, WINDOWS, ROWS], U8, name="xq_scales", align_bytes=64)
         w_words = [
-            keep.tile([P, WINDOWS, 2 * PHASE_FEATURES], U8, name="w_words%d" % i, align_bytes=64)
+            keep.tile([P, WINDOWS, 2 * MAX_PHASE * P], U8, name="w_words%d" % i, align_bytes=64)
             for i in range(2)
         ]
         w_scales = [
-            keep.tile([P, WINDOWS, PHASE_FEATURES], U8, name="w_scales%d" % i, align_bytes=64)
+            keep.tile([P, WINDOWS, MAX_PHASE * P], U8, name="w_scales%d" % i, align_bytes=64)
             for i in range(2)
         ]
         raw = {}
@@ -79,24 +93,25 @@ def tile_dendriticlayersilu_ffn_kernel(
         silu = {}
         weight = {}
         total = {}
+        den = {}
         inverse = {}
 
         def load_window(w):
-            x_raw = stage.tile([P, ROW_TILES, K_WINDOW], BF16, name="x_raw", bufs=3)
+            x_raw = stage.tile([P, ROW_TILES, K_WINDOW], BF16, name="x_raw", bufs=X_BUFS)
             nc.sync.dma_start(out=x_raw[:], in_=x_by_window[w])
             raw[w] = x_raw
 
         def load_weights(phase):
-            cols = slice(PHASE_FEATURES * phase, PHASE_FEATURES * (phase + 1))
-            byte_cols = slice(2 * PHASE_FEATURES * phase, 2 * PHASE_FEATURES * (phase + 1))
+            size = PHASE_SIZES[phase] * P
+            h0 = first_of[phase] * P
             for quadrant in range(4):
                 nc.sync.dma_start(
-                    out=w_scales[phase % 2][32 * quadrant : 32 * quadrant + 4, :, :].bitcast(I32),
-                    in_=scales_by_row[4 * quadrant : 4 * quadrant + 4, :, cols].bitcast(I32),
+                    out=w_scales[phase % 2][32 * quadrant : 32 * quadrant + 4, :, :size].bitcast(I32),
+                    in_=scales_by_row[4 * quadrant : 4 * quadrant + 4, :, h0 : h0 + size].bitcast(I32),
                 )
             nc.sync.dma_start(
-                out=w_words[phase % 2][:].bitcast(I32),
-                in_=words_by_partition[:, :, byte_cols].bitcast(I32),
+                out=w_words[phase % 2][:, :, : 2 * size].bitcast(I32),
+                in_=words_by_partition[:, :, 2 * h0 : 2 * (h0 + size)].bitcast(I32),
             )
 
         def quantise_window(w):
@@ -113,18 +128,19 @@ def tile_dendriticlayersilu_ffn_kernel(
                 side_by_side = grouped_words[:, 4 * P * pair : 4 * P * (pair + 1)].rearrange(
                     "p (n u) -> p n u", u=2
                 )
-                if pair == 0:
+                if pair == 0 or SCALAR_COPIES[w]:
                     nc.scalar.copy(out=side_by_side, in_=xt[:].rearrange("p u n -> p n u"))
                 else:
                     nc.vector.tensor_copy(out=side_by_side, in_=xt[:].rearrange("p u n -> p n u"))
             nc.vector.quantize_mx(
                 out=xq_codes[:, w, :].bitcast(FP8X4), scales=xq_scales[:, w, :], in_=grouped[:]
             )
-            if w + 3 < WINDOWS:
-                load_window(w + 3)
+            if w + X_BUFS < WINDOWS:
+                load_window(w + X_BUFS)
 
         def score_pass(block, w):
-            phase, place = divmod(block, PHASE_BLOCKS)
+            phase = phase_of[block]
+            place = place_of[block]
             bank = banks.tile([P, ROWS], F32, name="bank", tag="bank")
             nc.tensor.matmul_mx(
                 out=bank[:],
@@ -139,13 +155,16 @@ def tile_dendriticlayersilu_ffn_kernel(
 
         def peak_and_silu(block, w):
             if w == 0:
-                peak_tile = work.tile([P, ROWS], F32, name="peak", bufs=PHASE_BLOCKS)
+                peak_tile = work.tile([P, ROWS], F32, name="peak", bufs=MAX_PHASE)
                 peak[block] = peak_tile
-                silu_tile = work.tile([P, WINDOWS, ROWS], F32, name="silu", bufs=6)
+                silu_tile = work.tile([P, WINDOWS, ROWS], F32, name="silu", bufs=SILU_BUFS)
                 silu[block] = silu_tile
             bank = score_pass(block, w)
             if w == 0:
-                nc.vector.tensor_copy(out=peak[block][:], in_=bank[:])
+                if FIRST_ON_SCALAR and block >= 2:
+                    nc.scalar.copy(out=peak[block][:], in_=bank[:])
+                else:
+                    nc.vector.tensor_copy(out=peak[block][:], in_=bank[:])
             else:
                 nc.vector.tensor_tensor(
                     out=peak[block][:], in0=peak[block][:], in1=bank[:], op=ALU.max
@@ -154,7 +173,7 @@ def tile_dendriticlayersilu_ffn_kernel(
 
         def softmax_weight(block, w):
             if w == 0:
-                weight_tile = work.tile([P, WINDOWS, ROWS], F32, name="weight", bufs=3)
+                weight_tile = work.tile([P, WINDOWS, ROWS], F32, name="weight", bufs=WEIGHT_BUFS)
                 weight[block] = weight_tile
             bank = score_pass(block, w)
             nc.vector.tensor_tensor(
@@ -190,22 +209,37 @@ def tile_dendriticlayersilu_ffn_kernel(
                     stop=(w == WINDOWS - 1 and t == ROW_TILES - 1),
                 )
 
+        def small(name, bufs):
+            made = work.tile([P, ROW_TILES, P], F32, name=name, bufs=bufs)
+            return made
+
         def invert(block):
-            inverse_tile = work.tile([P, ROW_TILES, P], F32, name="inverse", bufs=3)
-            inverse[block] = inverse_tile
-            nc.vector.reciprocal(out=inverse_tile[:], in_=total["weight", block][:])
+            if block >= BLOCKS - TAIL:
+                inverse[block] = small("inverse", 3)
+                nc.vector.reciprocal(out=inverse[block][:], in_=total["weight", block][:])
+                return
+            if TAIL % 2 and block == BLOCKS - 1 - TAIL:
+                inverse[block] = small("inverse", 3)
+                nc.vector.reciprocal(out=inverse[block][:], in_=total["weight", block][:])
+                return
+            den[block] = small("den", 3)
+            nc.scalar.copy(out=den[block][:], in_=total["weight", block][:])
+            if block % 2 == 1:
+                a, b = block - 1, block
+                both = small("both", 2)
+                nc.gpsimd.tensor_tensor(out=both[:], in0=den[a][:], in1=den[b][:], op=ALU.mult)
+                nc.vector.reciprocal(out=both[:], in_=both[:])
+                for own, other in ((a, b), (b, a)):
+                    inverse[own] = small("inverse", 3)
+                    nc.gpsimd.tensor_tensor(
+                        out=inverse[own][:], in0=both[:], in1=den[other][:], op=ALU.mult
+                    )
 
         def finish(block):
-            result = work.tile([P, ROW_TILES, P], F32, name="result", bufs=3)
-            if block < BLOCKS - VECTOR_ENDS:
-                nc.scalar.copy(out=result[:], in_=total["product", block][:])
-                nc.gpsimd.tensor_tensor(
-                    out=result[:], in0=result[:], in1=inverse[block][:], op=ALU.mult
-                )
-            else:
-                nc.vector.tensor_tensor(
-                    out=result[:], in0=total["product", block][:], in1=inverse[block][:], op=ALU.mult
-                )
+            result = small("result", 3)
+            nc.vector.tensor_tensor(
+                out=result[:], in0=total["product", block][:], in1=inverse[block][:], op=ALU.mult
+            )
             nc.sync.dma_start(out=out_by_tile[:, :, P * block : P * (block + 1)], in_=result[:])
 
         for scales in w_scales:
@@ -216,7 +250,8 @@ def tile_dendriticlayersilu_ffn_kernel(
         load_window(0)
         load_window(1)
         load_weights(0)
-        load_window(2)
+        for w in range(2, X_BUFS):
+            load_window(w)
         quantise_window(0)
 
         closed = []
@@ -227,8 +262,8 @@ def tile_dendriticlayersilu_ffn_kernel(
                         quantise_window(w + 1)
                     peak_and_silu(block, w)
                 else:
-                    phase, place = divmod(block, PHASE_BLOCKS)
-                    if place == 0 and w == 0 and phase + 1 < PHASES:
+                    phase = phase_of[block]
+                    if place_of[block] == 0 and w == 0 and phase + 1 < PHASES:
                         load_weights(phase + 1)
                     softmax_weight(block, w)
                     if w % HALF == HALF - 1:

@@ -25,17 +25,22 @@ PHASE_SIZES = (2, 2, 2, 2, 2, 2, 2, 2)
 MAX_PHASE = max(PHASE_SIZES)
 PHASES = len(PHASE_SIZES)
 
-SLOT_PASSES = 4
-ADD_LAG = 24
+SLOT_PASSES = 2
+LAG_W = 12
+LAG_P = 32
 VECTOR_HALVES = 1
 SILU_BUFS = 6
 WEIGHT_BUFS = 3
 X_BUFS = 3
 PEAK_GROUP = 2
-SCALAR_COPIES = (0, 0, 0, 0, 0, 0, 0, 0)
+SCALAR_COPIES = (0, 1, 0, 1, 0, 1, 0, 1)
 FIRST_ON_SCALAR = 0
 V_FINALS = BLOCKS
-TAIL = 1
+PAIRS = 7
+RECIP_LAG = 1
+BOTH_LAG = 3
+VECTOR_ENDS = 0
+EARLY_WORDS = 1
 
 FLOPS = 2 * ROWS * FEATURES * WINDOWS * K_WINDOW
 
@@ -64,11 +69,11 @@ def tile_dendriticlayersilu_ffn_kernel(
         for g in range(0, size, PEAK_GROUP):
             passes.extend(("peak", block, w) for w in range(WINDOWS) for block in blocks[g : g + PEAK_GROUP])
         passes.extend(("weight", block, w) for block in blocks for w in range(WINDOWS))
-    additions = []
-    for pair in range(0, BLOCKS, 2):
-        for kind in ("weight", "product"):
-            for block in (pair, pair + 1):
-                additions.extend((block, kind, w) for w in range(WINDOWS))
+    due = {}
+    for position, (kind, block, w) in enumerate(passes):
+        if kind == "weight":
+            due.setdefault((position + LAG_W) // SLOT_PASSES, []).append((block, "weight", w))
+            due.setdefault((position + LAG_P) // SLOT_PASSES, []).append((block, "product", w))
 
     with ExitStack() as ctx:
         keep = ctx.enter_context(tc.tile_pool(name="keep", bufs=1))
@@ -109,10 +114,14 @@ def tile_dendriticlayersilu_ffn_kernel(
                     out=w_scales[phase % 2][32 * quadrant : 32 * quadrant + 4, :, :size].bitcast(I32),
                     in_=scales_by_row[4 * quadrant : 4 * quadrant + 4, :, h0 : h0 + size].bitcast(I32),
                 )
-            nc.sync.dma_start(
-                out=w_words[phase % 2][:, :, : 2 * size].bitcast(I32),
-                in_=words_by_partition[:, :, 2 * h0 : 2 * (h0 + size)].bitcast(I32),
-            )
+            cuts = (0, EARLY_WORDS, WINDOWS) if phase == 0 and EARLY_WORDS else (0, WINDOWS)
+            for w0, w1 in zip(cuts, cuts[1:]):
+                nc.sync.dma_start(
+                    out=w_words[phase % 2][:, w0:w1, : 2 * size].bitcast(I32),
+                    in_=words_by_partition[:, w0:w1, 2 * h0 : 2 * (h0 + size)].bitcast(I32),
+                )
+                if w0 == 0 and w1 < WINDOWS:
+                    load_window(1)
 
         def quantise_window(w):
             grouped = stage.tile([P, 4 * ROWS], BF16, name="grouped", align_bytes=64)
@@ -213,33 +222,27 @@ def tile_dendriticlayersilu_ffn_kernel(
             made = work.tile([P, ROW_TILES, P], F32, name=name, bufs=bufs)
             return made
 
-        def invert(block):
-            if block >= BLOCKS - TAIL:
+        def take_weight_sum(block):
+            if block >= 2 * PAIRS:
                 inverse[block] = small("inverse", 3)
                 nc.vector.reciprocal(out=inverse[block][:], in_=total["weight", block][:])
                 return
-            if TAIL % 2 and block == BLOCKS - 1 - TAIL:
-                inverse[block] = small("inverse", 3)
-                nc.vector.reciprocal(out=inverse[block][:], in_=total["weight", block][:])
-                return
-            den[block] = small("den", 3)
+            den[block] = small("den", 4)
             nc.scalar.copy(out=den[block][:], in_=total["weight", block][:])
             if block % 2 == 1:
-                a, b = block - 1, block
-                both = small("both", 2)
-                nc.gpsimd.tensor_tensor(out=both[:], in0=den[a][:], in1=den[b][:], op=ALU.mult)
-                nc.vector.reciprocal(out=both[:], in_=both[:])
-                for own, other in ((a, b), (b, a)):
-                    inverse[own] = small("inverse", 3)
-                    nc.gpsimd.tensor_tensor(
-                        out=inverse[own][:], in0=both[:], in1=den[other][:], op=ALU.mult
-                    )
+                later.setdefault(slot + BOTH_LAG, []).append(("both", block))
+                later.setdefault(slot + BOTH_LAG + RECIP_LAG, []).append(("recip", block))
 
         def finish(block):
             result = small("result", 3)
             nc.vector.tensor_tensor(
                 out=result[:], in0=total["product", block][:], in1=inverse[block][:], op=ALU.mult
             )
+            if block < 2 * PAIRS:
+                engine = nc.gpsimd if block < BLOCKS - VECTOR_ENDS else nc.vector
+                engine.tensor_tensor(
+                    out=result[:], in0=result[:], in1=den[block + 1 - 2 * (block % 2)][:], op=ALU.mult
+                )
             nc.sync.dma_start(out=out_by_tile[:, :, P * block : P * (block + 1)], in_=result[:])
 
         for scales in w_scales:
@@ -248,14 +251,19 @@ def tile_dendriticlayersilu_ffn_kernel(
         nc.vector.memset(warm[:], 0.0)
         nc.scalar.activation(out=warm[:], in_=warm[:], func=ACT.Silu)
         load_window(0)
-        load_window(1)
-        load_weights(0)
+        if EARLY_WORDS:
+            load_weights(0)
+        else:
+            load_window(1)
+            load_weights(0)
         for w in range(2, X_BUFS):
             load_window(w)
         quantise_window(0)
 
         closed = []
-        for start in range(0, len(passes) + ADD_LAG + SLOT_PASSES, SLOT_PASSES):
+        later = {}
+        for slot in range(max(due) + 2):
+            start = SLOT_PASSES * slot
             for kind, block, w in passes[start : start + SLOT_PASSES]:
                 if kind == "peak":
                     if block == 0 and w + 1 < WINDOWS:
@@ -270,11 +278,20 @@ def tile_dendriticlayersilu_ffn_kernel(
                         multiply(block, w // HALF)
             for block, kind in closed:
                 if kind == "weight":
-                    invert(block)
+                    take_weight_sum(block)
                 else:
                     finish(block)
             closed = []
-            for block, kind, w in additions[max(start - ADD_LAG, 0) : max(start - ADD_LAG + SLOT_PASSES, 0)]:
+            for what, block in later.get(slot, []):
+                if what == "both":
+                    inverse[block] = small("inverse", 3)
+                    inverse[block - 1] = inverse[block]
+                    nc.vector.tensor_tensor(
+                        out=inverse[block][:], in0=den[block - 1][:], in1=total["weight", block][:], op=ALU.mult
+                    )
+                else:
+                    nc.vector.reciprocal(out=inverse[block][:], in_=inverse[block][:])
+            for block, kind, w in due.get(slot, []):
                 add_window(block, kind, w)
                 if w == WINDOWS - 1:
                     closed.append((block, kind))

@@ -25,9 +25,9 @@ PHASE_SIZES = (2, 2, 2, 2, 2, 2, 2, 2)
 MAX_PHASE = max(PHASE_SIZES)
 PHASES = len(PHASE_SIZES)
 
-SLOT_PASSES = 2
-LAG_W = 12
-LAG_P = 32
+SLOT_PASSES = 4
+LAG_W = 10
+LAG_P = 36
 VECTOR_HALVES = 1
 SILU_BUFS = 6
 WEIGHT_BUFS = 3
@@ -38,7 +38,7 @@ FIRST_ON_SCALAR = 0
 V_FINALS = BLOCKS
 PAIRS = 7
 RECIP_LAG = 1
-BOTH_LAG = 3
+BOTH_LAG = 2
 VECTOR_ENDS = 0
 EARLY_WORDS = 1
 
@@ -226,6 +226,7 @@ def tile_dendriticlayersilu_ffn_kernel(
             if block >= 2 * PAIRS:
                 inverse[block] = small("inverse", 3)
                 nc.vector.reciprocal(out=inverse[block][:], in_=total["weight", block][:])
+                done.append(block)
                 return
             den[block] = small("den", 4)
             nc.scalar.copy(out=den[block][:], in_=total["weight", block][:])
@@ -262,7 +263,9 @@ def tile_dendriticlayersilu_ffn_kernel(
 
         closed = []
         later = {}
-        for slot in range(max(due) + 2):
+        waiting = []
+        done = []
+        for slot in range(max(due) + 8):
             start = SLOT_PASSES * slot
             for kind, block, w in passes[start : start + SLOT_PASSES]:
                 if kind == "peak":
@@ -280,17 +283,22 @@ def tile_dendriticlayersilu_ffn_kernel(
                 if kind == "weight":
                     take_weight_sum(block)
                 else:
-                    finish(block)
+                    waiting.append(block)
             closed = []
             for what, block in later.get(slot, []):
                 if what == "both":
                     inverse[block] = small("inverse", 3)
-                    inverse[block - 1] = inverse[block]
                     nc.vector.tensor_tensor(
                         out=inverse[block][:], in0=den[block - 1][:], in1=total["weight", block][:], op=ALU.mult
                     )
                 else:
                     nc.vector.reciprocal(out=inverse[block][:], in_=inverse[block][:])
+                    inverse[block - 1] = inverse[block]
+                    done.append(block - 1)
+                    done.append(block)
+            for block in [b for b in waiting if b in done]:
+                finish(block)
+                waiting.remove(block)
             for block, kind, w in due.get(slot, []):
                 add_window(block, kind, w)
                 if w == WINDOWS - 1:

@@ -37,6 +37,14 @@ SCALAR_COPIES = (0, 1, 0, 1, 0, 1, 0, 1)
 FIRST_ON_SCALAR = 0
 V_FINALS = BLOCKS
 PAIRS = 7
+PARTS = 2
+R_POS = 28
+R_OFF = 0
+PART_STEP = 1
+EXP_WINDOWS = 1
+SILU_START = 1
+FLOOR = -40.0
+SILU_PLACES = (0, 1, 2, 3)
 RECIP_LAG = 1
 BOTH_LAG = 2
 VECTOR_ENDS = 0
@@ -70,8 +78,11 @@ def tile_dendriticlayersilu_ffn_kernel(
             passes.extend(("peak", block, w) for w in range(WINDOWS) for block in blocks[g : g + PEAK_GROUP])
         passes.extend(("weight", block, w) for block in blocks for w in range(WINDOWS))
     due = {}
+    weights_at = {}
     for position, (kind, block, w) in enumerate(passes):
         if kind == "weight":
+            if w == 0:
+                weights_at[block] = position
             due.setdefault((position + LAG_W) // SLOT_PASSES, []).append((block, "weight", w))
             due.setdefault((position + LAG_P) // SLOT_PASSES, []).append((block, "product", w))
 
@@ -169,7 +180,12 @@ def tile_dendriticlayersilu_ffn_kernel(
                 silu_tile = work.tile([P, WINDOWS, ROWS], F32, name="silu", bufs=SILU_BUFS)
                 silu[block] = silu_tile
             bank = score_pass(block, w)
-            if w == 0:
+            if SILU_START and w <= 1 and (phase_of[block] > 0 or place_of[block] > 1) and place_of[block] in SILU_PLACES:
+                if w == 1:
+                    nc.vector.tensor_tensor(
+                        out=peak[block][:], in0=silu[block][:, 0, :], in1=bank[:], op=ALU.max
+                    )
+            elif w == 0:
                 if FIRST_ON_SCALAR and block >= 2:
                     nc.scalar.copy(out=peak[block][:], in_=bank[:])
                 else:
@@ -185,12 +201,22 @@ def tile_dendriticlayersilu_ffn_kernel(
                 weight_tile = work.tile([P, WINDOWS, ROWS], F32, name="weight", bufs=WEIGHT_BUFS)
                 weight[block] = weight_tile
             bank = score_pass(block, w)
-            nc.vector.tensor_tensor(
-                out=weight[block][:, w, :], in0=bank[:], in1=peak[block][:], op=ALU.subtract
-            )
-            nc.scalar.activation(
-                out=weight[block][:, w, :], in_=weight[block][:, w, :], func=ACT.Exp
-            )
+            if SILU_START and w == WINDOWS - 1:
+                nc.vector.scalar_tensor_tensor(
+                    out=weight[block][:, w, :],
+                    in0=bank[:],
+                    scalar=FLOOR,
+                    in1=peak[block][:],
+                    op0=ALU.max,
+                    op1=ALU.subtract,
+                )
+            else:
+                nc.vector.tensor_tensor(
+                    out=weight[block][:, w, :], in0=bank[:], in1=peak[block][:], op=ALU.subtract
+                )
+            if w % EXP_WINDOWS == EXP_WINDOWS - 1:
+                done_windows = weight[block][:, w + 1 - EXP_WINDOWS : w + 1, :]
+                nc.scalar.activation(out=done_windows, in_=done_windows, func=ACT.Exp)
 
         def multiply(block, half):
             ws = slice(HALF * half, HALF * (half + 1))
@@ -232,7 +258,8 @@ def tile_dendriticlayersilu_ffn_kernel(
             nc.scalar.copy(out=den[block][:], in_=total["weight", block][:])
             if block % 2 == 1:
                 later.setdefault(slot + BOTH_LAG, []).append(("both", block))
-                later.setdefault(slot + BOTH_LAG + RECIP_LAG, []).append(("recip", block))
+                for part in range(PARTS):
+                    later.setdefault(max(slot + BOTH_LAG + RECIP_LAG, (weights_at[block] + R_POS) // SLOT_PASSES) + (part + R_OFF) * PART_STEP, []).append(("recip%d" % part, block))
 
         def finish(block):
             result = small("result", 3)
@@ -265,7 +292,7 @@ def tile_dendriticlayersilu_ffn_kernel(
         later = {}
         waiting = []
         done = []
-        for slot in range(max(due) + 8):
+        for slot in range(max(due) + 12):
             start = SLOT_PASSES * slot
             for kind, block, w in passes[start : start + SLOT_PASSES]:
                 if kind == "peak":
@@ -292,10 +319,13 @@ def tile_dendriticlayersilu_ffn_kernel(
                         out=inverse[block][:], in0=den[block - 1][:], in1=total["weight", block][:], op=ALU.mult
                     )
                 else:
-                    nc.vector.reciprocal(out=inverse[block][:], in_=inverse[block][:])
-                    inverse[block - 1] = inverse[block]
-                    done.append(block - 1)
-                    done.append(block)
+                    part = int(what[5:])
+                    tiles = slice(ROW_TILES * part // PARTS, ROW_TILES * (part + 1) // PARTS)
+                    nc.vector.reciprocal(out=inverse[block][:, tiles, :], in_=inverse[block][:, tiles, :])
+                    if part == PARTS - 1:
+                        inverse[block - 1] = inverse[block]
+                        done.append(block - 1)
+                        done.append(block)
             for block in [b for b in waiting if b in done]:
                 finish(block)
                 waiting.remove(block)

@@ -26,27 +26,45 @@ MAX_PHASE = max(PHASE_SIZES)
 PHASES = len(PHASE_SIZES)
 
 SLOT_PASSES = 4
-LAG_W = 10
+LAG_W = 14
 LAG_P = 36
-VECTOR_HALVES = 1
+VECTOR_HALVES = 2
 SILU_BUFS = 6
 WEIGHT_BUFS = 3
-X_BUFS = 3
+X_BUFS = 5
 PEAK_GROUP = 2
 SCALAR_COPIES = (0, 1, 0, 1, 0, 1, 0, 1)
 FIRST_ON_SCALAR = 0
 V_FINALS = BLOCKS
 PAIRS = 7
-PARTS = 2
-R_POS = 28
+RESULT_BUFS = 5
+INVERSE_BUFS = 4
+DEN_BUFS = 4
+AHEAD = 3
+Q_AHEAD = 1
+Q_AFTER = -1
+T_AFTER = 1
+GROUPED_BUFS = 2
+PINNED = {mybir.EngineType.PE, mybir.EngineType.DVE, mybir.EngineType.Activation, mybir.EngineType.Pool}
+PARTS = 1
+R_POS = 0
+END_W = 8
+END_P = 24
+END_P2 = 36
+R_POS2 = 24
+TAIL_S = 1
+DEN_ON_VECTOR = (1,)
+V_DEFER = 1
 R_OFF = 0
 PART_STEP = 1
 EXP_WINDOWS = 1
 SILU_START = 1
+S_FIRST = 0
 FLOOR = -40.0
 SILU_PLACES = (0, 1, 2, 3)
 RECIP_LAG = 1
 BOTH_LAG = 2
+DEN_LAG = 0
 VECTOR_ENDS = 0
 EARLY_WORDS = 1
 
@@ -83,8 +101,11 @@ def tile_dendriticlayersilu_ffn_kernel(
         if kind == "weight":
             if w == 0:
                 weights_at[block] = position
-            due.setdefault((position + LAG_W) // SLOT_PASSES, []).append((block, "weight", w))
-            due.setdefault((position + LAG_P) // SLOT_PASSES, []).append((block, "product", w))
+            to_go = PHASES - 1 - phase_of[block]
+            lag_w = END_W if to_go == 0 else LAG_W
+            lag_p = END_P if to_go == 0 else END_P2 if to_go == 1 else LAG_P
+            due.setdefault((position + lag_w) // SLOT_PASSES, []).append((block, "weight", w))
+            due.setdefault((position + lag_p) // SLOT_PASSES, []).append((block, "product", w))
 
     with ExitStack() as ctx:
         keep = ctx.enter_context(tc.tile_pool(name="keep", bufs=1))
@@ -94,6 +115,7 @@ def tile_dendriticlayersilu_ffn_kernel(
 
         ident = keep.tile([P, P], F32, name="ident")
         warm = keep.tile([P, 1], F32, name="warm")
+        ctx.enter_context(tc.manual_schedule(engines=PINNED))
         xq_codes = keep.tile([P, WINDOWS, ROWS], U32, name="xq_codes", align_bytes=64)
         xq_scales = keep.tile([P, WINDOWS, ROWS], U8, name="xq_scales", align_bytes=64)
         w_words = [
@@ -105,6 +127,7 @@ def tile_dendriticlayersilu_ffn_kernel(
             for i in range(2)
         ]
         raw = {}
+        ready = {}
         peak = {}
         silu = {}
         weight = {}
@@ -134,8 +157,8 @@ def tile_dendriticlayersilu_ffn_kernel(
                 if w0 == 0 and w1 < WINDOWS:
                     load_window(1)
 
-        def quantise_window(w):
-            grouped = stage.tile([P, 4 * ROWS], BF16, name="grouped", align_bytes=64)
+        def turn_window(w):
+            grouped = stage.tile([P, 4 * ROWS], BF16, name="grouped", bufs=GROUPED_BUFS, align_bytes=64)
             grouped_words = grouped[:].bitcast(F32)
             for pair in range(2):
                 xt = banks.tile([P, 2, 2 * P], F32, name="xt", tag="bank")
@@ -152,11 +175,14 @@ def tile_dendriticlayersilu_ffn_kernel(
                     nc.scalar.copy(out=side_by_side, in_=xt[:].rearrange("p u n -> p n u"))
                 else:
                     nc.vector.tensor_copy(out=side_by_side, in_=xt[:].rearrange("p u n -> p n u"))
-            nc.vector.quantize_mx(
-                out=xq_codes[:, w, :].bitcast(FP8X4), scales=xq_scales[:, w, :], in_=grouped[:]
-            )
+            ready[w] = grouped
             if w + X_BUFS < WINDOWS:
                 load_window(w + X_BUFS)
+
+        def quantise_window(w):
+            nc.vector.quantize_mx(
+                out=xq_codes[:, w, :].bitcast(FP8X4), scales=xq_scales[:, w, :], in_=ready[w][:]
+            )
 
         def score_pass(block, w):
             phase = phase_of[block]
@@ -180,6 +206,9 @@ def tile_dendriticlayersilu_ffn_kernel(
                 silu_tile = work.tile([P, WINDOWS, ROWS], F32, name="silu", bufs=SILU_BUFS)
                 silu[block] = silu_tile
             bank = score_pass(block, w)
+            silu_first = S_FIRST and phase_of[block] >= S_FIRST
+            if silu_first:
+                nc.scalar.activation(out=silu[block][:, w, :], in_=bank[:], func=ACT.Silu)
             if SILU_START and w <= 1 and (phase_of[block] > 0 or place_of[block] > 1) and place_of[block] in SILU_PLACES:
                 if w == 1:
                     nc.vector.tensor_tensor(
@@ -194,7 +223,8 @@ def tile_dendriticlayersilu_ffn_kernel(
                 nc.vector.tensor_tensor(
                     out=peak[block][:], in0=peak[block][:], in1=bank[:], op=ALU.max
                 )
-            nc.scalar.activation(out=silu[block][:, w, :], in_=bank[:], func=ACT.Silu)
+            if not silu_first:
+                nc.scalar.activation(out=silu[block][:, w, :], in_=bank[:], func=ACT.Silu)
 
         def softmax_weight(block, w):
             if w == 0:
@@ -218,10 +248,12 @@ def tile_dendriticlayersilu_ffn_kernel(
                 done_windows = weight[block][:, w + 1 - EXP_WINDOWS : w + 1, :]
                 nc.scalar.activation(out=done_windows, in_=done_windows, func=ACT.Exp)
 
+        def is_late(block, half):
+            return 2 * (BLOCKS - 1 - block) + (1 - half) < VECTOR_HALVES
+
         def multiply(block, half):
             ws = slice(HALF * half, HALF * (half + 1))
-            late = 2 * (BLOCKS - 1 - block) + (1 - half) < VECTOR_HALVES
-            engine = nc.vector if late else nc.gpsimd
+            engine = nc.vector if is_late(block, half) else nc.gpsimd
             engine.tensor_tensor(
                 out=silu[block][:, ws, :],
                 in0=silu[block][:, ws, :],
@@ -250,19 +282,23 @@ def tile_dendriticlayersilu_ffn_kernel(
 
         def take_weight_sum(block):
             if block >= 2 * PAIRS:
-                inverse[block] = small("inverse", 3)
-                nc.vector.reciprocal(out=inverse[block][:], in_=total["weight", block][:])
-                done.append(block)
+                inverse[block] = small("inverse", INVERSE_BUFS)
+                if TAIL_S:
+                    nc.scalar.activation(out=inverse[block][:], in_=total["weight", block][:], func=ACT.Ln)
+                    if block == BLOCKS - 1:
+                        later.setdefault(slot + 1, []).append(("exp", block))
+                else:
+                    nc.vector.reciprocal(out=inverse[block][:], in_=total["weight", block][:])
+                    done.append(block)
                 return
-            den[block] = small("den", 4)
-            nc.scalar.copy(out=den[block][:], in_=total["weight", block][:])
+            later.setdefault(slot + DEN_LAG, []).append(("den", block))
             if block % 2 == 1:
-                later.setdefault(slot + BOTH_LAG, []).append(("both", block))
+                later.setdefault(slot + DEN_LAG + BOTH_LAG, []).append(("both", block))
                 for part in range(PARTS):
-                    later.setdefault(max(slot + BOTH_LAG + RECIP_LAG, (weights_at[block] + R_POS) // SLOT_PASSES) + (part + R_OFF) * PART_STEP, []).append(("recip%d" % part, block))
+                    later.setdefault(max(slot + DEN_LAG + BOTH_LAG + RECIP_LAG, (weights_at[block] + (R_POS2 if phase_of[block] == PHASES - 2 else R_POS)) // SLOT_PASSES) + (part + R_OFF) * PART_STEP, []).append(("recip%d" % part, block))
 
         def finish(block):
-            result = small("result", 3)
+            result = small("result", RESULT_BUFS)
             nc.vector.tensor_tensor(
                 out=result[:], in0=total["product", block][:], in1=inverse[block][:], op=ALU.mult
             )
@@ -286,26 +322,41 @@ def tile_dendriticlayersilu_ffn_kernel(
             load_weights(0)
         for w in range(2, X_BUFS):
             load_window(w)
-        quantise_window(0)
+        for w in range(AHEAD):
+            turn_window(w)
+            if w < (Q_AHEAD if Q_AFTER < 0 else 1):
+                quantise_window(w)
 
         closed = []
         later = {}
         waiting = []
+        deferred = []
         done = []
         for slot in range(max(due) + 12):
             start = SLOT_PASSES * slot
             for kind, block, w in passes[start : start + SLOT_PASSES]:
                 if kind == "peak":
-                    if block == 0 and w + 1 < WINDOWS:
-                        quantise_window(w + 1)
+                    if Q_AFTER < 0 and block == 0 and w + Q_AHEAD < WINDOWS:
+                        quantise_window(w + Q_AHEAD)
                     peak_and_silu(block, w)
+                    if block == Q_AFTER and w + 1 < WINDOWS:
+                        quantise_window(w + 1)
+                    if block == min(T_AFTER, PHASE_SIZES[0] - 1) and w + AHEAD < WINDOWS:
+                        turn_window(w + AHEAD)
                 else:
                     phase = phase_of[block]
                     if place_of[block] == 0 and w == 0 and phase + 1 < PHASES:
                         load_weights(phase + 1)
                     softmax_weight(block, w)
                     if w % HALF == HALF - 1:
-                        multiply(block, w // HALF)
+                        if V_DEFER and is_late(block, w // HALF):
+                            deferred.append((block, w // HALF))
+                        else:
+                            multiply(block, w // HALF)
+            if start + SLOT_PASSES >= len(passes):
+                for block, half in deferred:
+                    multiply(block, half)
+                deferred = []
             for block, kind in closed:
                 if kind == "weight":
                     take_weight_sum(block)
@@ -313,8 +364,18 @@ def tile_dendriticlayersilu_ffn_kernel(
                     waiting.append(block)
             closed = []
             for what, block in later.get(slot, []):
-                if what == "both":
-                    inverse[block] = small("inverse", 3)
+                if what == "exp":
+                    for b in (block - 1, block):
+                        nc.scalar.activation(out=inverse[b][:], in_=inverse[b][:], func=ACT.Exp, scale=-1.0)
+                        done.append(b)
+                elif what == "den":
+                    den[block] = small("den", DEN_BUFS)
+                    if block % 2 in DEN_ON_VECTOR:
+                        nc.vector.tensor_copy(out=den[block][:], in_=total["weight", block][:])
+                    else:
+                        nc.scalar.copy(out=den[block][:], in_=total["weight", block][:])
+                elif what == "both":
+                    inverse[block] = small("inverse", INVERSE_BUFS)
                     nc.vector.tensor_tensor(
                         out=inverse[block][:], in0=den[block - 1][:], in1=total["weight", block][:], op=ALU.mult
                     )

@@ -26,6 +26,7 @@ MAX_PHASE = max(PHASE_SIZES)
 PHASES = len(PHASE_SIZES)
 
 SLOT_PASSES = 4
+SLOT_ADDS = 8
 LAG_W = 14
 LAG_P = 36
 VECTOR_HALVES = 2
@@ -36,9 +37,11 @@ PEAK_GROUP = 2
 SCALAR_COPIES = (0, 1, 0, 1, 0, 1, 0, 1)
 FIRST_ON_SCALAR = 0
 V_FINALS = BLOCKS
-PAIRS = 7
+PAIRS = 6
+FOLD_LAST = 1
+FOLDED = ()
 RESULT_BUFS = 5
-INVERSE_BUFS = 4
+INVERSE_BUFS = 5
 DEN_BUFS = 4
 AHEAD = 3
 Q_AHEAD = 1
@@ -48,18 +51,22 @@ GROUPED_BUFS = 2
 PINNED = {mybir.EngineType.PE, mybir.EngineType.DVE, mybir.EngineType.Activation, mybir.EngineType.Pool}
 PARTS = 1
 R_POS = 0
+START_W = 14
+START_P = 36
 END_W = 8
 END_P = 24
 END_P2 = 36
 R_POS2 = 24
 TAIL_S = 1
-DEN_ON_VECTOR = (1,)
+DEN_ON_VECTOR = (0, 1)
 V_DEFER = 1
 R_OFF = 0
 PART_STEP = 1
 EXP_WINDOWS = 1
 SILU_START = 1
+SILU_FROM = 2
 S_FIRST = 0
+S_FIRST_UNTIL = 0
 FLOOR = -40.0
 SILU_PLACES = (0, 1, 2, 3)
 RECIP_LAG = 1
@@ -67,6 +74,7 @@ BOTH_LAG = 2
 DEN_LAG = 0
 VECTOR_ENDS = 0
 EARLY_WORDS = 1
+EARLY_X = 1
 
 FLOPS = 2 * ROWS * FEATURES * WINDOWS * K_WINDOW
 
@@ -89,6 +97,13 @@ def tile_dendriticlayersilu_ffn_kernel(
             phase_of.append(phase)
             place_of.append(place)
 
+    def last_window(block, kind):
+        if kind == "weight":
+            return WINDOWS - 1
+        if block >= BLOCKS - FOLD_LAST:
+            return HALF - 1
+        return WINDOWS - 3 if block in FOLDED else WINDOWS - 1
+
     passes = []
     for phase, size in enumerate(PHASE_SIZES):
         blocks = list(range(first_of[phase], first_of[phase] + size))
@@ -102,10 +117,11 @@ def tile_dendriticlayersilu_ffn_kernel(
             if w == 0:
                 weights_at[block] = position
             to_go = PHASES - 1 - phase_of[block]
-            lag_w = END_W if to_go == 0 else LAG_W
-            lag_p = END_P if to_go == 0 else END_P2 if to_go == 1 else LAG_P
+            lag_w = END_W if to_go == 0 else START_W if phase_of[block] == 0 else LAG_W
+            lag_p = END_P if to_go == 0 else END_P2 if to_go == 1 else START_P if phase_of[block] == 0 else LAG_P
             due.setdefault((position + lag_w) // SLOT_PASSES, []).append((block, "weight", w))
-            due.setdefault((position + lag_p) // SLOT_PASSES, []).append((block, "product", w))
+            if w < last_window(block, "product") + 1:
+                due.setdefault((position + lag_p) // SLOT_PASSES, []).append((block, "product", w))
 
     with ExitStack() as ctx:
         keep = ctx.enter_context(tc.tile_pool(name="keep", bufs=1))
@@ -155,7 +171,8 @@ def tile_dendriticlayersilu_ffn_kernel(
                     in_=words_by_partition[:, w0:w1, 2 * h0 : 2 * (h0 + size)].bitcast(I32),
                 )
                 if w0 == 0 and w1 < WINDOWS:
-                    load_window(1)
+                    for early in range(1, 1 + EARLY_X):
+                        load_window(early)
 
         def turn_window(w):
             grouped = stage.tile([P, 4 * ROWS], BF16, name="grouped", bufs=GROUPED_BUFS, align_bytes=64)
@@ -206,10 +223,10 @@ def tile_dendriticlayersilu_ffn_kernel(
                 silu_tile = work.tile([P, WINDOWS, ROWS], F32, name="silu", bufs=SILU_BUFS)
                 silu[block] = silu_tile
             bank = score_pass(block, w)
-            silu_first = S_FIRST and phase_of[block] >= S_FIRST
+            silu_first = (S_FIRST and phase_of[block] >= S_FIRST) or phase_of[block] < S_FIRST_UNTIL
             if silu_first:
                 nc.scalar.activation(out=silu[block][:, w, :], in_=bank[:], func=ACT.Silu)
-            if SILU_START and w <= 1 and (phase_of[block] > 0 or place_of[block] > 1) and place_of[block] in SILU_PLACES:
+            if SILU_START and w <= 1 and phase_of[block] >= SILU_FROM and place_of[block] in SILU_PLACES:
                 if w == 1:
                     nc.vector.tensor_tensor(
                         out=peak[block][:], in0=silu[block][:, 0, :], in1=bank[:], op=ALU.max
@@ -260,6 +277,10 @@ def tile_dendriticlayersilu_ffn_kernel(
                 in1=weight[block][:, ws, :],
                 op=ALU.mult,
             )
+            if half == 1 and block in FOLDED:
+                nc.gpsimd.tensor_tensor(
+                    out=silu[block][:, 4:6, :], in0=silu[block][:, 4:6, :], in1=silu[block][:, 6:8, :], op=ALU.add
+                )
 
         def add_window(block, kind, w):
             if w == 0:
@@ -273,7 +294,7 @@ def tile_dendriticlayersilu_ffn_kernel(
                     rhs=ident[:],
                     is_transpose=True,
                     start=(w == 0 and t == 0),
-                    stop=(w == WINDOWS - 1 and t == ROW_TILES - 1),
+                    stop=(w == last_window(block, kind) and t == ROW_TILES - 1),
                 )
 
         def small(name, bufs):
@@ -284,6 +305,16 @@ def tile_dendriticlayersilu_ffn_kernel(
             if block >= 2 * PAIRS:
                 inverse[block] = small("inverse", INVERSE_BUFS)
                 if TAIL_S:
+                    if block < BLOCKS - 2:
+                        den[block] = small("den", DEN_BUFS)
+                        if block % 2 in DEN_ON_VECTOR:
+                            nc.vector.tensor_copy(out=den[block][:], in_=total["weight", block][:])
+                        else:
+                            nc.scalar.copy(out=den[block][:], in_=total["weight", block][:])
+                        return
+                    if block == BLOCKS - 2:
+                        for b in range(2 * PAIRS, BLOCKS - 2):
+                            nc.scalar.activation(out=inverse[b][:], in_=den[b][:], func=ACT.Ln)
                     nc.scalar.activation(out=inverse[block][:], in_=total["weight", block][:], func=ACT.Ln)
                     if block == BLOCKS - 1:
                         later.setdefault(slot + 1, []).append(("exp", block))
@@ -320,7 +351,7 @@ def tile_dendriticlayersilu_ffn_kernel(
         else:
             load_window(1)
             load_weights(0)
-        for w in range(2, X_BUFS):
+        for w in range(1 + EARLY_X if EARLY_WORDS else 2, X_BUFS):
             load_window(w)
         for w in range(AHEAD):
             turn_window(w)
@@ -330,9 +361,10 @@ def tile_dendriticlayersilu_ffn_kernel(
         closed = []
         later = {}
         waiting = []
+        pending = []
         deferred = []
         done = []
-        for slot in range(max(due) + 12):
+        for slot in range(max(due) + 16):
             start = SLOT_PASSES * slot
             for kind, block, w in passes[start : start + SLOT_PASSES]:
                 if kind == "peak":
@@ -356,6 +388,10 @@ def tile_dendriticlayersilu_ffn_kernel(
             if start + SLOT_PASSES >= len(passes):
                 for block, half in deferred:
                     multiply(block, half)
+                    if half == 1 and block >= BLOCKS - FOLD_LAST:
+                        nc.vector.tensor_tensor(
+                            out=silu[block][:, :HALF, :], in0=silu[block][:, :HALF, :], in1=silu[block][:, HALF:, :], op=ALU.add
+                        )
                 deferred = []
             for block, kind in closed:
                 if kind == "weight":
@@ -365,7 +401,7 @@ def tile_dendriticlayersilu_ffn_kernel(
             closed = []
             for what, block in later.get(slot, []):
                 if what == "exp":
-                    for b in (block - 1, block):
+                    for b in range(2 * PAIRS, BLOCKS):
                         nc.scalar.activation(out=inverse[b][:], in_=inverse[b][:], func=ACT.Exp, scale=-1.0)
                         done.append(b)
                 elif what == "den":
@@ -390,7 +426,11 @@ def tile_dendriticlayersilu_ffn_kernel(
             for block in [b for b in waiting if b in done]:
                 finish(block)
                 waiting.remove(block)
-            for block, kind, w in due.get(slot, []):
+            pending.extend(due.get(slot, []))
+            count = SLOT_ADDS if start + SLOT_PASSES < len(passes) else len(pending)
+            now = pending[:count]
+            pending = pending[count:]
+            for block, kind, w in now:
                 add_window(block, kind, w)
-                if w == WINDOWS - 1:
+                if w == last_window(block, kind):
                     closed.append((block, kind))

from contextlib import ExitStack

import concourse.masks as masks
import concourse.mybir as mybir

F32 = mybir.dt.float32
BF16 = mybir.dt.bfloat16
I32 = mybir.dt.int32
U32 = mybir.dt.uint32
U8 = mybir.dt.uint8
FP8X4 = mybir.dt.float8_e4m3fn_x4
FP4X4 = mybir.dt.float4_e2m1fn_x4
ACT = mybir.ActivationFunctionType
ALU = mybir.AluOpType

P = 128
ROWS = 512
ROW_TILES = ROWS // P
FEATURES = 2048
WINDOWS = 8
HALF = WINDOWS // 2
K_WINDOW = 512
BLOCKS = FEATURES // P
PHASE_SIZES = (2, 2, 2, 2, 2, 2, 2, 2)
MAX_PHASE = max(PHASE_SIZES)
PHASES = len(PHASE_SIZES)

SLOT_PASSES = 4
SLOT_ADDS = 8
LAG_W = 14
LAG_P = 36
VECTOR_HALVES = 2
SILU_BUFS = 6
WEIGHT_BUFS = 3
X_BUFS = 5
PEAK_GROUP = 2
SCALAR_COPIES = (0, 1, 0, 1, 0, 1, 0, 1)
FIRST_ON_SCALAR = 0
V_FINALS = BLOCKS
PAIRS = 6
FOLD_LAST = 1
FOLDED = ()
RESULT_BUFS = 5
INVERSE_BUFS = 5
DEN_BUFS = 4
AHEAD = 3
Q_AHEAD = 1
Q_AFTER = -1
T_AFTER = 1
GROUPED_BUFS = 2
PINNED = {mybir.EngineType.PE, mybir.EngineType.DVE, mybir.EngineType.Activation, mybir.EngineType.Pool}
PARTS = 1
R_POS = 0
START_W = 14
START_P = 36
END_W = 8
END_P = 24
END_P2 = 36
R_POS2 = 24
TAIL_S = 1
DEN_ON_VECTOR = (0, 1)
V_DEFER = 1
R_OFF = 0
PART_STEP = 1
EXP_WINDOWS = 1
SILU_START = 1
SILU_FROM = 2
S_FIRST = 0
S_FIRST_UNTIL = 0
FLOOR = -40.0
SILU_PLACES = (0, 1, 2, 3)
RECIP_LAG = 1
BOTH_LAG = 2
DEN_LAG = 0
VECTOR_ENDS = 0
EARLY_WORDS = 1
EARLY_X = 1

FLOPS = 2 * ROWS * FEATURES * WINDOWS * K_WINDOW


def tile_dendriticlayersilu_ffn_kernel(
    tc, x, template_flat_words, template_flat_scales, out
):
    nc = tc.nc
    x_by_window = x.rearrange("(t p) (w k) -> w p t k", p=P, k=K_WINDOW)
    words_by_partition = template_flat_words.rearrange("g p b -> p g b")
    scales_by_row = template_flat_scales.rearrange("g r h -> r g h")
    out_by_tile = out.rearrange("(t p) h -> p t h", p=P)

    phase_of = []
    place_of = []
    first_of = []
    for phase, size in enumerate(PHASE_SIZES):
        first_of.append(len(phase_of))
        for place in range(size):
            phase_of.append(phase)
            place_of.append(place)

    def last_window(block, kind):
        if kind == "weight":
            return WINDOWS - 1
        if block >= BLOCKS - FOLD_LAST:
            return HALF - 1
        return WINDOWS - 3 if block in FOLDED else WINDOWS - 1

    passes = []
    for phase, size in enumerate(PHASE_SIZES):
        blocks = list(range(first_of[phase], first_of[phase] + size))
        for g in range(0, size, PEAK_GROUP):
            passes.extend(("peak", block, w) for w in range(WINDOWS) for block in blocks[g : g + PEAK_GROUP])
        passes.extend(("weight", block, w) for block in blocks for w in range(WINDOWS))
    due = {}
    weights_at = {}
    for position, (kind, block, w) in enumerate(passes):
        if kind == "weight":
            if w == 0:
                weights_at[block] = position
            to_go = PHASES - 1 - phase_of[block]
            lag_w = END_W if to_go == 0 else START_W if phase_of[block] == 0 else LAG_W
            lag_p = END_P if to_go == 0 else END_P2 if to_go == 1 else START_P if phase_of[block] == 0 else LAG_P
            due.setdefault((position + lag_w) // SLOT_PASSES, []).append((block, "weight", w))
            if w < last_window(block, "product") + 1:
                due.setdefault((position + lag_p) // SLOT_PASSES, []).append((block, "product", w))

    with ExitStack() as ctx:
        keep = ctx.enter_context(tc.tile_pool(name="keep", bufs=1))
        stage = ctx.enter_context(tc.tile_pool(name="stage", bufs=2))
        work = ctx.enter_context(tc.tile_pool(name="work", bufs=2))
        banks = ctx.enter_context(tc.psum_pool(name="banks", bufs=8))

        ident = keep.tile([P, P], F32, name="ident")
        warm = keep.tile([P, 1], F32, name="warm")
        ctx.enter_context(tc.manual_schedule(engines=PINNED))
        xq_codes = keep.tile([P, WINDOWS, ROWS], U32, name="xq_codes", align_bytes=64)
        xq_scales = keep.tile([P, WINDOWS, ROWS], U8, name="xq_scales", align_bytes=64)
        w_words = [
            keep.tile([P, WINDOWS, 2 * MAX_PHASE * P], U8, name="w_words%d" % i, align_bytes=64)
            for i in range(2)
        ]
        w_scales = [
            keep.tile([P, WINDOWS, MAX_PHASE * P], U8, name="w_scales%d" % i, align_bytes=64)
            for i in range(2)
        ]
        raw = {}
        ready = {}
        peak = {}
        silu = {}
        weight = {}
        total = {}
        den = {}
        inverse = {}

        def load_window(w):
            x_raw = stage.tile([P, ROW_TILES, K_WINDOW], BF16, name="x_raw", bufs=X_BUFS)
            nc.sync.dma_start(out=x_raw[:], in_=x_by_window[w])
            raw[w] = x_raw

        def load_weights(phase):
            size = PHASE_SIZES[phase] * P
            h0 = first_of[phase] * P
            for quadrant in range(4):
                nc.sync.dma_start(
                    out=w_scales[phase % 2][32 * quadrant : 32 * quadrant + 4, :, :size].bitcast(I32),
                    in_=scales_by_row[4 * quadrant : 4 * quadrant + 4, :, h0 : h0 + size].bitcast(I32),
                )
            cuts = (0, EARLY_WORDS, WINDOWS) if phase == 0 and EARLY_WORDS else (0, WINDOWS)
            for w0, w1 in zip(cuts, cuts[1:]):
                nc.sync.dma_start(
                    out=w_words[phase % 2][:, w0:w1, : 2 * size].bitcast(I32),
                    in_=words_by_partition[:, w0:w1, 2 * h0 : 2 * (h0 + size)].bitcast(I32),
                )
                if w0 == 0 and w1 < WINDOWS:
                    for early in range(1, 1 + EARLY_X):
                        load_window(early)

        def turn_window(w):
            grouped = stage.tile([P, 4 * ROWS], BF16, name="grouped", bufs=GROUPED_BUFS, align_bytes=64)
            grouped_words = grouped[:].bitcast(F32)
            for pair in range(2):
                xt = banks.tile([P, 2, 2 * P], F32, name="xt", tag="bank")
                for u in range(2):
                    for i in range(2):
                        words = raw[w][:, 2 * pair + i, :].bitcast(F32)
                        nc.tensor.transpose(
                            xt[:, u, P * i : P * (i + 1)], words[:, u : K_WINDOW // 2 : 2], ident[:]
                        )
                side_by_side = grouped_words[:, 4 * P * pair : 4 * P * (pair + 1)].rearrange(
                    "p (n u) -> p n u", u=2
                )
                if pair == 0 or SCALAR_COPIES[w]:
                    nc.scalar.copy(out=side_by_side, in_=xt[:].rearrange("p u n -> p n u"))
                else:
                    nc.vector.tensor_copy(out=side_by_side, in_=xt[:].rearrange("p u n -> p n u"))
            ready[w] = grouped
            if w + X_BUFS < WINDOWS:
                load_window(w + X_BUFS)

        def quantise_window(w):
            nc.vector.quantize_mx(
                out=xq_codes[:, w, :].bitcast(FP8X4), scales=xq_scales[:, w, :], in_=ready[w][:]
            )

        def score_pass(block, w):
            phase = phase_of[block]
            place = place_of[block]
            bank = banks.tile([P, ROWS], F32, name="bank", tag="bank")
            nc.tensor.matmul_mx(
                out=bank[:],
                lhsT=w_words[phase % 2][:, w, 2 * P * place : 2 * P * (place + 1)].bitcast(FP4X4),
                lhsT_scale=w_scales[phase % 2][:, w, P * place : P * (place + 1)],
                rhs=xq_codes[:, w, :].bitcast(FP8X4),
                rhs_scale=xq_scales[:, w, :],
                start=True,
                stop=True,
            )
            return bank

        def peak_and_silu(block, w):
            if w == 0:
                peak_tile = work.tile([P, ROWS], F32, name="peak", bufs=MAX_PHASE)
                peak[block] = peak_tile
                silu_tile = work.tile([P, WINDOWS, ROWS], F32, name="silu", bufs=SILU_BUFS)
                silu[block] = silu_tile
            bank = score_pass(block, w)
            silu_first = (S_FIRST and phase_of[block] >= S_FIRST) or phase_of[block] < S_FIRST_UNTIL
            if silu_first:
                nc.scalar.activation(out=silu[block][:, w, :], in_=bank[:], func=ACT.Silu)
            if SILU_START and w <= 1 and phase_of[block] >= SILU_FROM and place_of[block] in SILU_PLACES:
                if w == 1:
                    nc.vector.tensor_tensor(
                        out=peak[block][:], in0=silu[block][:, 0, :], in1=bank[:], op=ALU.max
                    )
            elif w == 0:
                if FIRST_ON_SCALAR and block >= 2:
                    nc.scalar.copy(out=peak[block][:], in_=bank[:])
                else:
                    nc.vector.tensor_copy(out=peak[block][:], in_=bank[:])
            else:
                nc.vector.tensor_tensor(
                    out=peak[block][:], in0=peak[block][:], in1=bank[:], op=ALU.max
                )
            if not silu_first:
                nc.scalar.activation(out=silu[block][:, w, :], in_=bank[:], func=ACT.Silu)

        def softmax_weight(block, w):
            if w == 0:
                weight_tile = work.tile([P, WINDOWS, ROWS], F32, name="weight", bufs=WEIGHT_BUFS)
                weight[block] = weight_tile
            bank = score_pass(block, w)
            if SILU_START and w == WINDOWS - 1:
                nc.vector.scalar_tensor_tensor(
                    out=weight[block][:, w, :],
                    in0=bank[:],
                    scalar=FLOOR,
                    in1=peak[block][:],
                    op0=ALU.max,
                    op1=ALU.subtract,
                )
            else:
                nc.vector.tensor_tensor(
                    out=weight[block][:, w, :], in0=bank[:], in1=peak[block][:], op=ALU.subtract
                )
            if w % EXP_WINDOWS == EXP_WINDOWS - 1:
                done_windows = weight[block][:, w + 1 - EXP_WINDOWS : w + 1, :]
                nc.scalar.activation(out=done_windows, in_=done_windows, func=ACT.Exp)

        def is_late(block, half):
            return 2 * (BLOCKS - 1 - block) + (1 - half) < VECTOR_HALVES

        def multiply(block, half):
            ws = slice(HALF * half, HALF * (half + 1))
            engine = nc.vector if is_late(block, half) else nc.gpsimd
            engine.tensor_tensor(
                out=silu[block][:, ws, :],
                in0=silu[block][:, ws, :],
                in1=weight[block][:, ws, :],
                op=ALU.mult,
            )
            if half == 1 and block in FOLDED:
                nc.gpsimd.tensor_tensor(
                    out=silu[block][:, 4:6, :], in0=silu[block][:, 4:6, :], in1=silu[block][:, 6:8, :], op=ALU.add
                )

        def add_window(block, kind, w):
            if w == 0:
                bank = banks.tile([P, ROW_TILES, P], F32, name="window_sum", tag="bank")
                total[kind, block] = bank
            terms = weight[block] if kind == "weight" else silu[block]
            for t in range(ROW_TILES):
                nc.tensor.matmul(
                    out=total[kind, block][:, t, :],
                    lhsT=terms[:, w, P * t : P * (t + 1)],
                    rhs=ident[:],
                    is_transpose=True,
                    start=(w == 0 and t == 0),
                    stop=(w == last_window(block, kind) and t == ROW_TILES - 1),
                )

        def small(name, bufs):
            made = work.tile([P, ROW_TILES, P], F32, name=name, bufs=bufs)
            return made

        def take_weight_sum(block):
            if block >= 2 * PAIRS:
                inverse[block] = small("inverse", INVERSE_BUFS)
                if TAIL_S:
                    if block < BLOCKS - 2:
                        den[block] = small("den", DEN_BUFS)
                        if block % 2 in DEN_ON_VECTOR:
                            nc.vector.tensor_copy(out=den[block][:], in_=total["weight", block][:])
                        else:
                            nc.scalar.copy(out=den[block][:], in_=total["weight", block][:])
                        return
                    if block == BLOCKS - 2:
                        for b in range(2 * PAIRS, BLOCKS - 2):
                            nc.scalar.activation(out=inverse[b][:], in_=den[b][:], func=ACT.Ln)
                    nc.scalar.activation(out=inverse[block][:], in_=total["weight", block][:], func=ACT.Ln)
                    if block == BLOCKS - 1:
                        later.setdefault(slot + 1, []).append(("exp", block))
                else:
                    nc.vector.reciprocal(out=inverse[block][:], in_=total["weight", block][:])
                    done.append(block)
                return
            later.setdefault(slot + DEN_LAG, []).append(("den", block))
            if block % 2 == 1:
                later.setdefault(slot + DEN_LAG + BOTH_LAG, []).append(("both", block))
                for part in range(PARTS):
                    later.setdefault(max(slot + DEN_LAG + BOTH_LAG + RECIP_LAG, (weights_at[block] + (R_POS2 if phase_of[block] == PHASES - 2 else R_POS)) // SLOT_PASSES) + (part + R_OFF) * PART_STEP, []).append(("recip%d" % part, block))

        def finish(block):
            result = small("result", RESULT_BUFS)
            nc.vector.tensor_tensor(
                out=result[:], in0=total["product", block][:], in1=inverse[block][:], op=ALU.mult
            )
            if block < 2 * PAIRS:
                engine = nc.gpsimd if block < BLOCKS - VECTOR_ENDS else nc.vector
                engine.tensor_tensor(
                    out=result[:], in0=result[:], in1=den[block + 1 - 2 * (block % 2)][:], op=ALU.mult
                )
            nc.sync.dma_start(out=out_by_tile[:, :, P * block : P * (block + 1)], in_=result[:])

        for scales in w_scales:
            nc.vector.memset(scales[:].bitcast(I32), 0)
        masks.make_identity(nc, ident[:])
        nc.vector.memset(warm[:], 0.0)
        nc.scalar.activation(out=warm[:], in_=warm[:], func=ACT.Silu)
        load_window(0)
        if EARLY_WORDS:
            load_weights(0)
        else:
            load_window(1)
            load_weights(0)
        for w in range(1 + EARLY_X if EARLY_WORDS else 2, X_BUFS):
            load_window(w)
        for w in range(AHEAD):
            turn_window(w)
            if w < (Q_AHEAD if Q_AFTER < 0 else 1):
                quantise_window(w)

        closed = []
        later = {}
        waiting = []
        pending = []
        deferred = []
        done = []
        for slot in range(max(due) + 16):
            start = SLOT_PASSES * slot
            for kind, block, w in passes[start : start + SLOT_PASSES]:
                if kind == "peak":
                    if Q_AFTER < 0 and block == 0 and w + Q_AHEAD < WINDOWS:
                        quantise_window(w + Q_AHEAD)
                    peak_and_silu(block, w)
                    if block == Q_AFTER and w + 1 < WINDOWS:
                        quantise_window(w + 1)
                    if block == min(T_AFTER, PHASE_SIZES[0] - 1) and w + AHEAD < WINDOWS:
                        turn_window(w + AHEAD)
                else:
                    phase = phase_of[block]
                    if place_of[block] == 0 and w == 0 and phase + 1 < PHASES:
                        load_weights(phase + 1)
                    softmax_weight(block, w)
                    if w % HALF == HALF - 1:
                        if V_DEFER and is_late(block, w // HALF):
                            deferred.append((block, w // HALF))
                        else:
                            multiply(block, w // HALF)
            if start + SLOT_PASSES >= len(passes):
                for block, half in deferred:
                    multiply(block, half)
                    if half == 1 and block >= BLOCKS - FOLD_LAST:
                        nc.vector.tensor_tensor(
                            out=silu[block][:, :HALF, :], in0=silu[block][:, :HALF, :], in1=silu[block][:, HALF:, :], op=ALU.add
                        )
                deferred = []
            for block, kind in closed:
                if kind == "weight":
                    take_weight_sum(block)
                else:
                    waiting.append(block)
            closed = []
            for what, block in later.get(slot, []):
                if what == "exp":
                    for b in range(2 * PAIRS, BLOCKS):
                        nc.scalar.activation(out=inverse[b][:], in_=inverse[b][:], func=ACT.Exp, scale=-1.0)
                        done.append(b)
                elif what == "den":
                    den[block] = small("den", DEN_BUFS)
                    if block % 2 in DEN_ON_VECTOR:
                        nc.vector.tensor_copy(out=den[block][:], in_=total["weight", block][:])
                    else:
                        nc.scalar.copy(out=den[block][:], in_=total["weight", block][:])
                elif what == "both":
                    inverse[block] = small("inverse", INVERSE_BUFS)
                    nc.vector.tensor_tensor(
                        out=inverse[block][:], in0=den[block - 1][:], in1=total["weight", block][:], op=ALU.mult
                    )
                else:
                    part = int(what[5:])
                    tiles = slice(ROW_TILES * part // PARTS, ROW_TILES * (part + 1) // PARTS)
                    nc.vector.reciprocal(out=inverse[block][:, tiles, :], in_=inverse[block][:, tiles, :])
                    if part == PARTS - 1:
                        inverse[block - 1] = inverse[block]
                        done.append(block - 1)
                        done.append(block)
            for block in [b for b in waiting if b in done]:
                finish(block)
                waiting.remove(block)
            pending.extend(due.get(slot, []))
            count = SLOT_ADDS if start + SLOT_PASSES < len(passes) else len(pending)
            now = pending[:count]
            pending = pending[count:]
            for block, kind, w in now:
                add_window(block, kind, w)
                if w == last_window(block, kind):
                    closed.append((block, kind))
